import numpy as np
import ml_dtypes


def mxq(x, axis, fmt="e4m3"):
    dtype, down = {"e4m3": (ml_dtypes.float8_e4m3fn, 7), "e5m2": (ml_dtypes.float8_e5m2, 14)}[fmt]
    v = np.moveaxis(np.asarray(x, np.float32).astype(ml_dtypes.bfloat16).astype(np.float64), axis, -1)
    blocks = v.reshape(v.shape[:-1] + (-1, 32))
    amax = np.abs(blocks).max(-1, keepdims=True)
    byte = np.maximum(np.where(amax > 0, np.frexp(amax)[1] - 1 + 127, 0) - down, 1)
    scale = np.exp2(byte - 127.0)
    codes = (blocks / scale).astype(np.float32).astype(dtype).astype(np.float64)
    return np.moveaxis((codes * scale).reshape(v.shape), -1, axis)


WIDE = False


def mx_kscale(k):
    if not WIDE:
        return np.ones(k)
    levels = np.array([10, -10, 5, -5, 0])
    a = np.random.permutation(np.resize(levels, k // 512 * 4)).reshape(k // 512, 4)
    idx = np.arange(k)
    return np.exp2(a[idx // 512, idx % 128 // 32])


BF16 = ml_dtypes.bfloat16


def bf(x):
    return np.asarray(x, np.float32).astype(BF16)


def f64(x):
    return np.asarray(x).astype(np.float64)


B, N, W, H, D = 1, 8, 512, 8, 128


def setup_inputs():
    s = mx_kscale(W)[:, None]
    m = np.random.uniform(0.2, 1.0, (N, N))
    return {"k_feat": bf(np.maximum(np.random.standard_normal((B, H, N, W, D)) * 0.5, 0.0) * s),
            "v": bf(np.random.standard_normal((B, H, N, W, D)) * 0.5 / s),
            "w_piece": bf(m / m.sum(axis=0, keepdims=True))}


def reference(k_feat, v, w_piece):
    kq = mxq(f64(k_feat), 3, "e4m3")
    vq = mxq(f64(v), 3, "e4m3")
    kv = kq.transpose(0, 1, 2, 4, 3) @ vq
    wp = f64(w_piece)
    return (wp[None, None, :, :, None, None] * kv[:, :, None, :, :, :]).sum(axis=3)

@@ -1,0 +1,261 @@
+from contextlib import ExitStack
+
+import concourse.mybir as mybir
+from concourse.masks import make_identity
+
+BF16 = mybir.dt.bfloat16
+F32 = mybir.dt.float32
+U32 = mybir.dt.uint32
+U8 = mybir.dt.uint8
+FP8X4 = mybir.dt.float8_e4m3fn_x4
+MULT = mybir.AluOpType.mult
+ADD = mybir.AluOpType.add
+COPY = mybir.ActivationFunctionType.Copy
+AXIS_X = mybir.AxisListType.X
+
+P = 128
+HEADS = 8
+WINDOWS = 8
+QUAD = 4
+PACK = 4
+D = 128
+ROW = PACK * D
+SLICE = 16
+SLICES = 6
+TE_COLS = SLICE * SLICES
+HALF = SLICES // 2
+LEAD = 3
+AHEAD = 12
+R_AHEAD = 3
+
+FLOPS = 2 * HEADS * WINDOWS * 512 * D * D + 2 * HEADS * WINDOWS * WINDOWS * D * D
+
+
+def tile_mhla_pa_kernel(tc, k_feat, v, w_piece, out):
+    nc = tc.nc
+    with ExitStack() as ctx:
+        const = ctx.enter_context(tc.tile_pool(name="const", bufs=1))
+        rawp = ctx.enter_context(tc.tile_pool(name="rawp", bufs=2 * AHEAD))
+        grpp = ctx.enter_context(tc.tile_pool(name="grpp", bufs=8))
+        mxp = ctx.enter_context(tc.tile_pool(name="mxp", bufs=8))
+        accp = ctx.enter_context(tc.tile_pool(name="accp", bufs=1))
+        ysbp = ctx.enter_context(tc.tile_pool(name="ysbp", bufs=4))
+        psum_v = ctx.enter_context(tc.psum_pool(name="psum_v", bufs=2))
+        psum_s = ctx.enter_context(tc.psum_pool(name="psum_s", bufs=2))
+        psum_t = ctx.enter_context(tc.psum_pool(name="psum_t", bufs=4))
+        ctx.enter_context(tc.manual_schedule())
+
+        order = [(0, j) for j in range(LEAD)]
+        for j in range(WINDOWS):
+            order.append((1, j))
+            if j + LEAD < WINDOWS:
+                order.append((0, j + LEAD))
+        n_units = len(order)
+        last_te = order.index((0, WINDOWS - 1))
+
+        raws = {}
+        grps = {}
+        words = {}
+        banks = {}
+
+        def load(n):
+            q, j = order[n]
+            for name, src in (("k", k_feat), ("v", v)):
+                raw = rawp.tile([P, QUAD, ROW], BF16, tag="raw", name="raw_%s%d" % (name, n))
+                nc.sync.dma_start(
+                    out=raw[:],
+                    in_=src[0, QUAD * q : QUAD * (q + 1), j].rearrange("h (p t) d -> p h (t d)", t=PACK),
+                )
+                raws[(name, n)] = raw
+
+        def regroup(n):
+            for name in ("k", "v"):
+                raw = raws[(name, n)]
+                grp = grpp.tile([P, QUAD, ROW], BF16, tag="grp", name="grp_%s%d" % (name, n), align_bytes=64)
+                grps[(name, n)] = grp
+                if name == "k":
+                    for h in range(QUAD):
+                        nc.scalar.copy(
+                            out=grp[:, h, :].rearrange("p (c i t) -> p c t i", i=4, t=PACK),
+                            in_=raw[:, h, :].rearrange("p (t c i) -> p c t i", i=4, t=PACK),
+                        )
+                elif n < 2:
+                    nc.vector.tensor_copy(
+                        out=grp[:].rearrange("p h (c i t) -> p h c t i", i=4, t=PACK),
+                        in_=raw[:].rearrange("p h (t c i) -> p h c t i", i=4, t=PACK),
+                    )
+                else:
+                    nc.gpsimd.tensor_scalar(
+                        out=grp[:].rearrange("p h (d t) -> p h d t", t=PACK),
+                        in0=raw[:].rearrange("p h (t d) -> p h d t", t=PACK),
+                        scalar1=1.0,
+                        scalar2=0.0,
+                        op0=MULT,
+                        op1=ADD,
+                    )
+            if n + AHEAD < n_units:
+                load(n + AHEAD)
+
+        def quantise(n):
+            for name in ("k", "v"):
+                codes = mxp.tile([P, QUAD * D], U32, tag="codes", name="codes_%s%d" % (name, n), align_bytes=64)
+                scales = mxp.tile([P, QUAD * D], U8, tag="scales", name="scales_%s%d" % (name, n), align_bytes=64)
+                nc.vector.quantize_mx(
+                    out=codes[:].bitcast(FP8X4),
+                    scales=scales[:],
+                    in_=grps[(name, n)][:].rearrange("p h x -> p (h x)"),
+                )
+                words[(name, n)] = (codes, scales)
+
+        def passes_into(n, bank):
+            for h in range(QUAD):
+                cols = slice(h * D, (h + 1) * D)
+                nc.tensor.matmul_mx(
+                    out=bank[:, h, :],
+                    lhsT=words[("k", n)][0][:, cols].bitcast(FP8X4),
+                    lhsT_scale=words[("k", n)][1][:, cols],
+                    rhs=words[("v", n)][0][:, cols].bitcast(FP8X4),
+                    rhs_scale=words[("v", n)][1][:, cols],
+                    start=True,
+                    stop=True,
+                )
+
+        def weight(i, j):
+            return w_f[:, i * WINDOWS + j : i * WINDOWS + j + 1]
+
+        def passes(n):
+            q, j = order[n]
+            lo = TE_COLS if q == 0 else 0
+            if q == 0 or j == 0:
+                for_scalar = psum_s.tile([P, QUAD, D], F32, tag="for_scalar", name="for_scalar%d" % n)
+                passes_into(n, for_scalar)
+                if q == 0:
+                    nc.scalar.copy(
+                        out=states[:, :, :, j, :],
+                        in_=for_scalar[:].rearrange("p h (s r) -> p h s r", r=SLICE)[:, :, 0:SLICES, :],
+                    )
+                if j == 0:
+                    for i in range(WINDOWS):
+                        nc.scalar.activation(
+                            out=acc[q][:, i, :, lo:D], in_=for_scalar[:, :, lo:D], func=COPY, scale=weight(i, 0)
+                        )
+            if j > 0:
+                for_vector = psum_v.tile([P, QUAD, D], F32, tag="for_vector", name="for_vector%d" % n)
+                passes_into(n, for_vector)
+                banks[n] = for_vector
+
+        def vector_mix(n):
+            q, j = order[n]
+            lo = TE_COLS if q == 0 else 0
+            if j == 0:
+                return
+            for i in range(WINDOWS):
+                nc.vector.scalar_tensor_tensor(
+                    out=acc[q][:, i, :, lo:D],
+                    in0=banks[n][:, :, lo:D],
+                    scalar=weight(i, j),
+                    in1=acc[q][:, i, :, lo:D],
+                    op0=MULT,
+                    op1=ADD,
+                )
+                if q == 1 and j == WINDOWS - 1:
+                    nc.sync.dma_start(
+                        out=out[0, QUAD : 2 * QUAD, i].rearrange("h d e -> d h e"), in_=acc[1][:, i, :, :]
+                    )
+
+        flipped = {}
+
+        def flip(h):
+            for half in range(2):
+                y_ps = psum_t.tile([P, HALF, P], F32, tag="t", name="y_ps%d_%d" % (h, half))
+                for k in range(HALF):
+                    nc.tensor.transpose(
+                        y_ps[:, k, :], states[:, h, half * HALF + k, :, :].rearrange("p j r -> p (j r)"), ident[:]
+                    )
+                y_sb = ysbp.tile([P, HALF, P], F32, tag="y_sb", name="y_sb%d_%d" % (h, half))
+                nc.scalar.copy(out=y_sb[:], in_=y_ps[:])
+                flipped[(h, half)] = y_sb
+
+        def te_mix(h):
+            for half in range(2):
+                o_ps = psum_t.tile([P, HALF, P], F32, tag="t", name="o_ps%d_%d" % (h, half))
+                for k in range(HALF):
+                    nc.tensor.matmul(
+                        out=o_ps[:, k, :],
+                        lhsT=flipped[(h, half)][:, k, :],
+                        rhs=kron[:].rearrange("p i r -> p (i r)"),
+                        start=True,
+                        stop=True,
+                    )
+                lo = half * HALF * SLICE
+                nc.scalar.copy(
+                    out=acc[0][:, :, h, lo : lo + HALF * SLICE].rearrange("p i (s r) -> p i s r", r=SLICE),
+                    in_=o_ps[:].rearrange("p s (i r) -> p i s r", r=SLICE),
+                )
+
+        for n in range(AHEAD):
+            load(n)
+
+        w_bf = const.tile([P, WINDOWS * WINDOWS], BF16)
+        nc.scalar.dma_start(out=w_bf[:], in_=w_piece.rearrange("i j -> (i j)").partition_broadcast(P))
+        w_f = const.tile([P, WINDOWS * WINDOWS], F32)
+        nc.vector.tensor_copy(out=w_f[:], in_=w_bf[:])
+        ident = const.tile([P, P], F32)
+        make_identity(nc, ident[:])
+        window_of = const.tile([P, WINDOWS], F32)
+        nc.vector.tensor_reduce(
+            out=window_of[:], in_=ident[:].rearrange("p (j r) -> p j r", r=SLICE), axis=AXIS_X, op=ADD
+        )
+        column_of = const.tile([P, SLICE], F32)
+        nc.vector.tensor_reduce(
+            out=column_of[:], in_=ident[:].rearrange("p (j r) -> p r j", r=SLICE), axis=AXIS_X, op=ADD
+        )
+        picked = const.tile([P, WINDOWS, WINDOWS], F32)
+        nc.vector.tensor_tensor(
+            out=picked[:],
+            in0=w_f[:].rearrange("p (i j) -> p i j", j=WINDOWS),
+            in1=window_of[:].unsqueeze(1).to_broadcast([P, WINDOWS, WINDOWS]),
+            op=MULT,
+        )
+        w_own = const.tile([P, WINDOWS], F32)
+        nc.vector.tensor_reduce(out=w_own[:], in_=picked[:], axis=AXIS_X, op=ADD)
+        kron = const.tile([P, WINDOWS, SLICE], F32)
+        nc.vector.tensor_tensor(
+            out=kron[:],
+            in0=w_own[:].unsqueeze(2).to_broadcast([P, WINDOWS, SLICE]),
+            in1=column_of[:].unsqueeze(1).to_broadcast([P, WINDOWS, SLICE]),
+            op=MULT,
+        )
+
+        acc = [
+            accp.tile([P, WINDOWS, QUAD, D], F32, name="acc_te"),
+            accp.tile([P, WINDOWS, QUAD, D], F32, name="acc_ve"),
+        ]
+        states = accp.tile([P, QUAD, SLICES, WINDOWS, SLICE], F32, name="states")
+
+        regroup(0)
+        quantise(0)
+        passes(0)
+        for n in range(1, R_AHEAD):
+            regroup(n)
+
+        tail_step = 0
+        stored = 0
+        for n in range(n_units):
+            if n + R_AHEAD < n_units:
+                regroup(n + R_AHEAD)
+            if n + 1 < n_units:
+                quantise(n + 1)
+                passes(n + 1)
+            vector_mix(n)
+            if n + 1 >= last_te:
+                for rep in range(2):
+                    if tail_step < QUAD:
+                        flip(tail_step)
+                    if 1 <= tail_step <= QUAD:
+                        te_mix(tail_step - 1)
+                    tail_step += 1
+            if n >= last_te:
+                while stored < min(tail_step - 1, QUAD):
+                    nc.sync.dma_start(out=out[0, stored].rearrange("i d e -> d i e"), in_=acc[0][:, :, stored, :])
+                    stored += 1

@@ -24,9 +24,9 @@ SLICE = 16
 SLICES = 6
 TE_COLS = SLICE * SLICES
 HALF = SLICES // 2
-LEAD = 3
 AHEAD = 12
-R_AHEAD = 3
+TE = 0
+VE = 1
 
 FLOPS = 2 * HEADS * WINDOWS * 512 * D * D + 2 * HEADS * WINDOWS * WINDOWS * D * D
 
@@ -36,22 +36,22 @@ def tile_mhla_pa_kernel(tc, k_feat, v, w_piece, out):
     with ExitStack() as ctx:
         const = ctx.enter_context(tc.tile_pool(name="const", bufs=1))
         rawp = ctx.enter_context(tc.tile_pool(name="rawp", bufs=2 * AHEAD))
-        grpp = ctx.enter_context(tc.tile_pool(name="grpp", bufs=8))
+        grp_a = ctx.enter_context(tc.tile_pool(name="grp_a", bufs=2))
+        grp_b = ctx.enter_context(tc.tile_pool(name="grp_b", bufs=8))
         mxp = ctx.enter_context(tc.tile_pool(name="mxp", bufs=8))
         accp = ctx.enter_context(tc.tile_pool(name="accp", bufs=1))
         ysbp = ctx.enter_context(tc.tile_pool(name="ysbp", bufs=4))
-        psum_v = ctx.enter_context(tc.psum_pool(name="psum_v", bufs=2))
-        psum_s = ctx.enter_context(tc.psum_pool(name="psum_s", bufs=2))
-        psum_t = ctx.enter_context(tc.psum_pool(name="psum_t", bufs=4))
+        psum_v = ctx.enter_context(tc.psum_pool(name="psum_v", bufs=3))
+        psum_s = ctx.enter_context(tc.psum_pool(name="psum_s", bufs=5))
         ctx.enter_context(tc.manual_schedule())
 
-        order = [(0, j) for j in range(LEAD)]
-        for j in range(WINDOWS):
-            order.append((1, j))
-            if j + LEAD < WINDOWS:
-                order.append((0, j + LEAD))
-        n_units = len(order)
-        last_te = order.index((0, WINDOWS - 1))
+        steps = [[(VE, 0)], [(VE, 1)]]
+        for a in range(WINDOWS // 2):
+            steps.append([(TE, 2 * a), (TE, 2 * a + 1), (VE, a + 2)])
+        steps.append([(VE, WINDOWS - 2)])
+        steps.append([(VE, WINDOWS - 1)])
+        units = [unit for step in steps for unit in step]
+        te_end = 1 + WINDOWS // 2
 
         raws = {}
         grps = {}
@@ -59,63 +59,85 @@ def tile_mhla_pa_kernel(tc, k_feat, v, w_piece, out):
         banks = {}
 
         def load(n):
-            q, j = order[n]
+            q, j = units[n]
             for name, src in (("k", k_feat), ("v", v)):
-                raw = rawp.tile([P, QUAD, ROW], BF16, tag="raw", name="raw_%s%d" % (name, n))
+                raw = rawp.tile([P, QUAD, ROW], BF16, tag="raw", name="raw_%s%d%d" % (name, q, j))
                 nc.sync.dma_start(
                     out=raw[:],
                     in_=src[0, QUAD * q : QUAD * (q + 1), j].rearrange("h (p t) d -> p h (t d)", t=PACK),
                 )
-                raws[(name, n)] = raw
+                raws[(name, q, j)] = raw
 
-        def regroup(n):
-            for name in ("k", "v"):
-                raw = raws[(name, n)]
-                grp = grpp.tile([P, QUAD, ROW], BF16, tag="grp", name="grp_%s%d" % (name, n), align_bytes=64)
-                grps[(name, n)] = grp
-                if name == "k":
-                    for h in range(QUAD):
-                        nc.scalar.copy(
-                            out=grp[:, h, :].rearrange("p (c i t) -> p c t i", i=4, t=PACK),
-                            in_=raw[:, h, :].rearrange("p (t c i) -> p c t i", i=4, t=PACK),
-                        )
-                elif n < 2:
-                    nc.vector.tensor_copy(
-                        out=grp[:].rearrange("p h (c i t) -> p h c t i", i=4, t=PACK),
-                        in_=raw[:].rearrange("p h (t c i) -> p h c t i", i=4, t=PACK),
-                    )
-                else:
-                    nc.gpsimd.tensor_scalar(
-                        out=grp[:].rearrange("p h (d t) -> p h d t", t=PACK),
-                        in0=raw[:].rearrange("p h (t d) -> p h d t", t=PACK),
-                        scalar1=1.0,
-                        scalar2=0.0,
-                        op0=MULT,
-                        op1=ADD,
-                    )
-            if n + AHEAD < n_units:
-                load(n + AHEAD)
+        def late_k(q, j):
+            return q == VE and j >= WINDOWS - 2
 
-        def quantise(n):
-            for name in ("k", "v"):
-                codes = mxp.tile([P, QUAD * D], U32, tag="codes", name="codes_%s%d" % (name, n), align_bytes=64)
-                scales = mxp.tile([P, QUAD * D], U8, tag="scales", name="scales_%s%d" % (name, n), align_bytes=64)
-                nc.vector.quantize_mx(
-                    out=codes[:].bitcast(FP8X4),
-                    scales=scales[:],
-                    in_=grps[(name, n)][:].rearrange("p h x -> p (h x)"),
+        def regroup(name, q, j):
+            raw = raws[(name, q, j)]
+            fixed = q == VE and not (name == "k" and late_k(q, j))
+            pool = grp_a if fixed else grp_b
+            grp = pool.tile([P, QUAD, ROW], BF16, tag="grp", name="grp_%s%d%d" % (name, q, j), align_bytes=64)
+            grps[(name, q, j)] = grp
+            if q == TE or (name == "k" and (j < 2 or late_k(q, j))):
+                for h in range(QUAD):
+                    nc.scalar.copy(
+                        out=grp[:, h, :].rearrange("p (c i t) -> p c t i", i=4, t=PACK),
+                        in_=raw[:, h, :].rearrange("p (t c i) -> p c t i", i=4, t=PACK),
+                    )
+            elif j < 2:
+                nc.vector.tensor_copy(
+                    out=grp[:].rearrange("p h (c i t) -> p h c t i", i=4, t=PACK),
+                    in_=raw[:].rearrange("p h (t c i) -> p h c t i", i=4, t=PACK),
                 )
-                words[(name, n)] = (codes, scales)
+            else:
+                nc.gpsimd.tensor_scalar(
+                    out=grp[:].rearrange("p h (d t) -> p h d t", t=PACK),
+                    in0=raw[:].rearrange("p h (t d) -> p h d t", t=PACK),
+                    scalar1=1.0,
+                    scalar2=0.0,
+                    op0=MULT,
+                    op1=ADD,
+                )
 
-        def passes_into(n, bank):
+        def regroup_early(s):
+            q, j = steps[s][0]
+            if q == TE:
+                regroup("k", q, j)
+                regroup("v", q, j)
+            elif late_k(q, j):
+                regroup("k", q, j)
+
+        def regroup_late(s):
+            for index, (q, j) in enumerate(steps[s]):
+                if q == TE and index > 0:
+                    regroup("k", q, j)
+                    regroup("v", q, j)
+                if q == VE:
+                    if not late_k(q, j):
+                        regroup("k", q, j)
+                    regroup("v", q, j)
+                n = units.index((q, j))
+                if n + AHEAD < len(units):
+                    load(n + AHEAD)
+
+        def quantise(name, q, j):
+            codes = mxp.tile([P, QUAD * D], U32, tag="codes", name="codes_%s%d%d" % (name, q, j), align_bytes=64)
+            scales = mxp.tile([P, QUAD * D], U8, tag="scales", name="scales_%s%d%d" % (name, q, j), align_bytes=64)
+            nc.vector.quantize_mx(
+                out=codes[:].bitcast(FP8X4),
+                scales=scales[:],
+                in_=grps[(name, q, j)][:].rearrange("p h x -> p (h x)"),
+            )
+            words[(name, q, j)] = (codes, scales)
+
+        def passes_into(q, j, bank):
             for h in range(QUAD):
                 cols = slice(h * D, (h + 1) * D)
                 nc.tensor.matmul_mx(
                     out=bank[:, h, :],
-                    lhsT=words[("k", n)][0][:, cols].bitcast(FP8X4),
-                    lhsT_scale=words[("k", n)][1][:, cols],
-                    rhs=words[("v", n)][0][:, cols].bitcast(FP8X4),
-                    rhs_scale=words[("v", n)][1][:, cols],
+                    lhsT=words[("k", q, j)][0][:, cols].bitcast(FP8X4),
+                    lhsT_scale=words[("k", q, j)][1][:, cols],
+                    rhs=words[("v", q, j)][0][:, cols].bitcast(FP8X4),
+                    rhs_scale=words[("v", q, j)][1][:, cols],
                     start=True,
                     stop=True,
                 )
@@ -123,51 +145,62 @@ def tile_mhla_pa_kernel(tc, k_feat, v, w_piece, out):
         def weight(i, j):
             return w_f[:, i * WINDOWS + j : i * WINDOWS + j + 1]
 
-        def passes(n):
-            q, j = order[n]
-            lo = TE_COLS if q == 0 else 0
-            if q == 0 or j == 0:
-                for_scalar = psum_s.tile([P, QUAD, D], F32, tag="for_scalar", name="for_scalar%d" % n)
-                passes_into(n, for_scalar)
-                if q == 0:
-                    nc.scalar.copy(
-                        out=states[:, :, :, j, :],
-                        in_=for_scalar[:].rearrange("p h (s r) -> p h s r", r=SLICE)[:, :, 0:SLICES, :],
-                    )
+        def quantise_and_multiply(q, j):
+            for name in ("k", "v") if q == TE else ("v", "k"):
+                quantise(name, q, j)
+            if q == TE:
+                for_scalar = psum_s.tile([P, QUAD, D], F32, tag="s", name="for_scalar%d" % j)
+                passes_into(q, j, for_scalar)
+                nc.scalar.copy(
+                    out=states[:, :, :, j, :],
+                    in_=for_scalar[:].rearrange("p h (s r) -> p h s r", r=SLICE)[:, :, 0:SLICES, :],
+                )
                 if j == 0:
                     for i in range(WINDOWS):
                         nc.scalar.activation(
-                            out=acc[q][:, i, :, lo:D], in_=for_scalar[:, :, lo:D], func=COPY, scale=weight(i, 0)
+                            out=acc[TE][:, i, :, TE_COLS:D],
+                            in_=for_scalar[:, :, TE_COLS:D],
+                            func=COPY,
+                            scale=weight(i, 0),
                         )
-            if j > 0:
-                for_vector = psum_v.tile([P, QUAD, D], F32, tag="for_vector", name="for_vector%d" % n)
-                passes_into(n, for_vector)
-                banks[n] = for_vector
+            if q == VE or j > 0:
+                for_vector = psum_v.tile([P, QUAD, D], F32, tag="v", name="for_vector%d%d" % (q, j))
+                passes_into(q, j, for_vector)
+                banks[(q, j)] = for_vector
 
-        def vector_mix(n):
-            q, j = order[n]
-            lo = TE_COLS if q == 0 else 0
-            if j == 0:
+        def vector_mix(q, j):
+            lo = TE_COLS if q == TE else 0
+            if q == TE and j == 0:
                 return
             for i in range(WINDOWS):
-                nc.vector.scalar_tensor_tensor(
-                    out=acc[q][:, i, :, lo:D],
-                    in0=banks[n][:, :, lo:D],
-                    scalar=weight(i, j),
-                    in1=acc[q][:, i, :, lo:D],
-                    op0=MULT,
-                    op1=ADD,
-                )
-                if q == 1 and j == WINDOWS - 1:
+                if j == 0:
+                    nc.vector.tensor_scalar(
+                        out=acc[q][:, i, :, lo:D],
+                        in0=banks[(q, j)][:, :, lo:D],
+                        scalar1=weight(i, j),
+                        scalar2=0.0,
+                        op0=MULT,
+                        op1=ADD,
+                    )
+                else:
+                    nc.vector.scalar_tensor_tensor(
+                        out=acc[q][:, i, :, lo:D],
+                        in0=banks[(q, j)][:, :, lo:D],
+                        scalar=weight(i, j),
+                        in1=acc[q][:, i, :, lo:D],
+                        op0=MULT,
+                        op1=ADD,
+                    )
+                if q == VE and j == WINDOWS - 1:
                     nc.sync.dma_start(
-                        out=out[0, QUAD : 2 * QUAD, i].rearrange("h d e -> d h e"), in_=acc[1][:, i, :, :]
+                        out=out[0, QUAD : 2 * QUAD, i].rearrange("h d e -> d h e"), in_=acc[VE][:, i, :, :]
                     )
 
         flipped = {}
 
         def flip(h):
             for half in range(2):
-                y_ps = psum_t.tile([P, HALF, P], F32, tag="t", name="y_ps%d_%d" % (h, half))
+                y_ps = psum_s.tile([P, HALF, P], F32, tag="s", name="y_ps%d_%d" % (h, half))
                 for k in range(HALF):
                     nc.tensor.transpose(
                         y_ps[:, k, :], states[:, h, half * HALF + k, :, :].rearrange("p j r -> p (j r)"), ident[:]
@@ -178,7 +211,7 @@ def tile_mhla_pa_kernel(tc, k_feat, v, w_piece, out):
 
         def te_mix(h):
             for half in range(2):
-                o_ps = psum_t.tile([P, HALF, P], F32, tag="t", name="o_ps%d_%d" % (h, half))
+                o_ps = psum_s.tile([P, HALF, P], F32, tag="s", name="o_ps%d_%d" % (h, half))
                 for k in range(HALF):
                     nc.tensor.matmul(
                         out=o_ps[:, k, :],
@@ -189,7 +222,7 @@ def tile_mhla_pa_kernel(tc, k_feat, v, w_piece, out):
                     )
                 lo = half * HALF * SLICE
                 nc.scalar.copy(
-                    out=acc[0][:, :, h, lo : lo + HALF * SLICE].rearrange("p i (s r) -> p i s r", r=SLICE),
+                    out=acc[TE][:, :, h, lo : lo + HALF * SLICE].rearrange("p i (s r) -> p i s r", r=SLICE),
                     in_=o_ps[:].rearrange("p s (i r) -> p i s r", r=SLICE),
                 )
 
@@ -233,29 +266,22 @@ def tile_mhla_pa_kernel(tc, k_feat, v, w_piece, out):
         ]
         states = accp.tile([P, QUAD, SLICES, WINDOWS, SLICE], F32, name="states")
 
-        regroup(0)
-        quantise(0)
-        passes(0)
-        for n in range(1, R_AHEAD):
-            regroup(n)
-
-        tail_step = 0
-        stored = 0
-        for n in range(n_units):
-            if n + R_AHEAD < n_units:
-                regroup(n + R_AHEAD)
-            if n + 1 < n_units:
-                quantise(n + 1)
-                passes(n + 1)
-            vector_mix(n)
-            if n + 1 >= last_te:
-                for rep in range(2):
-                    if tail_step < QUAD:
-                        flip(tail_step)
-                    if 1 <= tail_step <= QUAD:
-                        te_mix(tail_step - 1)
-                    tail_step += 1
-            if n >= last_te:
-                while stored < min(tail_step - 1, QUAD):
-                    nc.sync.dma_start(out=out[0, stored].rearrange("i d e -> d i e"), in_=acc[0][:, :, stored, :])
-                    stored += 1
+        regroup_late(0)
+        for s, step in enumerate(steps):
+            if s + 1 < len(steps):
+                regroup_early(s + 1)
+            for q, j in step:
+                quantise_and_multiply(q, j)
+            if s + 1 < len(steps):
+                regroup_late(s + 1)
+            tail_steps = range(0, 3) if s == te_end else range(3, QUAD + 1) if s == te_end + 1 else range(0)
+            for t in tail_steps:
+                if t < QUAD:
+                    flip(t)
+                if t >= 1:
+                    te_mix(t - 1)
+            for q, j in step:
+                vector_mix(q, j)
+            for t in tail_steps:
+                if t >= 1:
+                    nc.sync.dma_start(out=out[0, t - 1].rearrange("i d e -> d i e"), in_=acc[TE][:, :, t - 1, :])

@@ -45,13 +45,13 @@ def tile_mhla_pa_kernel(tc, k_feat, v, w_piece, out):
         psum_s = ctx.enter_context(tc.psum_pool(name="psum_s", bufs=5))
         ctx.enter_context(tc.manual_schedule())
 
-        steps = [[(VE, 0)], [(VE, 1)]]
+        steps = [[(VE, 0)], [(VE, 1)], [(VE, 2)]]
         for a in range(WINDOWS // 2):
-            steps.append([(TE, 2 * a), (TE, 2 * a + 1), (VE, a + 2)])
-        steps.append([(VE, WINDOWS - 2)])
+            steps.append([(VE, a + 3), (TE, 2 * a), (TE, 2 * a + 1)])
         steps.append([(VE, WINDOWS - 1)])
         units = [unit for step in steps for unit in step]
-        te_end = 1 + WINDOWS // 2
+        te_end = 2 + WINDOWS // 2
+        ring_units = [step[-1] for step in steps[1:]]
 
         raws = {}
         grps = {}
@@ -68,22 +68,20 @@ def tile_mhla_pa_kernel(tc, k_feat, v, w_piece, out):
                 )
                 raws[(name, q, j)] = raw
 
-        def late_k(q, j):
-            return q == VE and j >= WINDOWS - 2
-
         def regroup(name, q, j):
             raw = raws[(name, q, j)]
-            fixed = q == VE and not (name == "k" and late_k(q, j))
-            pool = grp_a if fixed else grp_b
+            in_ring = (q, j) in ring_units
+            pool = grp_a if in_ring else grp_b
             grp = pool.tile([P, QUAD, ROW], BF16, tag="grp", name="grp_%s%d%d" % (name, q, j), align_bytes=64)
             grps[(name, q, j)] = grp
-            if q == TE or (name == "k" and (j < 2 or late_k(q, j))):
+            start = q == VE and j < 2
+            if (start and name == "k") or not (start or in_ring):
                 for h in range(QUAD):
                     nc.scalar.copy(
                         out=grp[:, h, :].rearrange("p (c i t) -> p c t i", i=4, t=PACK),
                         in_=raw[:, h, :].rearrange("p (t c i) -> p c t i", i=4, t=PACK),
                     )
-            elif j < 2:
+            elif start:
                 nc.vector.tensor_copy(
                     out=grp[:].rearrange("p h (c i t) -> p h c t i", i=4, t=PACK),
                     in_=raw[:].rearrange("p h (t c i) -> p h c t i", i=4, t=PACK),
@@ -98,23 +96,21 @@ def tile_mhla_pa_kernel(tc, k_feat, v, w_piece, out):
                     op1=ADD,
                 )
 
+        def regroup_unit(q, j):
+            regroup("k", q, j)
+            regroup("v", q, j)
+
         def regroup_early(s):
-            q, j = steps[s][0]
-            if q == TE:
-                regroup("k", q, j)
-                regroup("v", q, j)
-            elif late_k(q, j):
-                regroup("k", q, j)
+            if len(steps[s]) > 1:
+                regroup_unit(*steps[s][0])
 
         def regroup_late(s):
-            for index, (q, j) in enumerate(steps[s]):
-                if q == TE and index > 0:
-                    regroup("k", q, j)
+            for q, j in steps[s][1:] if len(steps[s]) > 1 else steps[s]:
+                if (q, j) == (VE, 1):
                     regroup("v", q, j)
-                if q == VE:
-                    if not late_k(q, j):
-                        regroup("k", q, j)
-                    regroup("v", q, j)
+                else:
+                    regroup_unit(q, j)
+            for q, j in steps[s]:
                 n = units.index((q, j))
                 if n + AHEAD < len(units):
                     load(n + AHEAD)
@@ -146,51 +142,40 @@ def tile_mhla_pa_kernel(tc, k_feat, v, w_piece, out):
             return w_f[:, i * WINDOWS + j : i * WINDOWS + j + 1]
 
         def quantise_and_multiply(q, j):
-            for name in ("k", "v") if q == TE else ("v", "k"):
+            lo = TE_COLS if q == TE else 0
+            for name in ("v", "k") if (q, j) in ring_units else ("k", "v"):
                 quantise(name, q, j)
-            if q == TE:
-                for_scalar = psum_s.tile([P, QUAD, D], F32, tag="s", name="for_scalar%d" % j)
+            if q == TE or j == 0:
+                for_scalar = psum_s.tile([P, QUAD, D], F32, tag="s", name="for_scalar%d%d" % (q, j))
                 passes_into(q, j, for_scalar)
-                nc.scalar.copy(
-                    out=states[:, :, :, j, :],
-                    in_=for_scalar[:].rearrange("p h (s r) -> p h s r", r=SLICE)[:, :, 0:SLICES, :],
-                )
+                if q == TE:
+                    nc.scalar.copy(
+                        out=states[:, :, :, j, :],
+                        in_=for_scalar[:].rearrange("p h (s r) -> p h s r", r=SLICE)[:, :, 0:SLICES, :],
+                    )
                 if j == 0:
                     for i in range(WINDOWS):
                         nc.scalar.activation(
-                            out=acc[TE][:, i, :, TE_COLS:D],
-                            in_=for_scalar[:, :, TE_COLS:D],
-                            func=COPY,
-                            scale=weight(i, 0),
+                            out=acc[q][:, i, :, lo:D], in_=for_scalar[:, :, lo:D], func=COPY, scale=weight(i, 0)
                         )
-            if q == VE or j > 0:
+            if j > 0:
                 for_vector = psum_v.tile([P, QUAD, D], F32, tag="v", name="for_vector%d%d" % (q, j))
                 passes_into(q, j, for_vector)
                 banks[(q, j)] = for_vector
 
         def vector_mix(q, j):
             lo = TE_COLS if q == TE else 0
-            if q == TE and j == 0:
+            if j == 0:
                 return
             for i in range(WINDOWS):
-                if j == 0:
-                    nc.vector.tensor_scalar(
-                        out=acc[q][:, i, :, lo:D],
-                        in0=banks[(q, j)][:, :, lo:D],
-                        scalar1=weight(i, j),
-                        scalar2=0.0,
-                        op0=MULT,
-                        op1=ADD,
-                    )
-                else:
-                    nc.vector.scalar_tensor_tensor(
-                        out=acc[q][:, i, :, lo:D],
-                        in0=banks[(q, j)][:, :, lo:D],
-                        scalar=weight(i, j),
-                        in1=acc[q][:, i, :, lo:D],
-                        op0=MULT,
-                        op1=ADD,
-                    )
+                nc.vector.scalar_tensor_tensor(
+                    out=acc[q][:, i, :, lo:D],
+                    in0=banks[(q, j)][:, :, lo:D],
+                    scalar=weight(i, j),
+                    in1=acc[q][:, i, :, lo:D],
+                    op0=MULT,
+                    op1=ADD,
+                )
                 if q == VE and j == WINDOWS - 1:
                     nc.sync.dma_start(
                         out=out[0, QUAD : 2 * QUAD, i].rearrange("h d e -> d h e"), in_=acc[VE][:, i, :, :]
@@ -267,6 +252,7 @@ def tile_mhla_pa_kernel(tc, k_feat, v, w_piece, out):
         states = accp.tile([P, QUAD, SLICES, WINDOWS, SLICE], F32, name="states")
 
         regroup_late(0)
+        regroup("k", VE, 1)
         for s, step in enumerate(steps):
             if s + 1 < len(steps):
                 regroup_early(s + 1)
@@ -280,8 +266,15 @@ def tile_mhla_pa_kernel(tc, k_feat, v, w_piece, out):
                     flip(t)
                 if t >= 1:
                     te_mix(t - 1)
+                    if s > te_end:
+                        nc.scalar.dma_start(
+                            out=out[0, t - 1].rearrange("i d e -> d i e"), in_=acc[TE][:, :, t - 1, :]
+                        )
             for q, j in step:
                 vector_mix(q, j)
-            for t in tail_steps:
-                if t >= 1:
-                    nc.sync.dma_start(out=out[0, t - 1].rearrange("i d e -> d i e"), in_=acc[TE][:, :, t - 1, :])
+            if s == te_end:
+                for t in tail_steps:
+                    if t >= 1:
+                        nc.sync.dma_start(
+                            out=out[0, t - 1].rearrange("i d e -> d i e"), in_=acc[TE][:, :, t - 1, :]
+                        )

@@ -20,13 +20,23 @@ QUAD = 4
 PACK = 4
 D = 128
 ROW = PACK * D
+COLS = QUAD * D
 SLICE = 16
-SLICES = 6
+SLICES = 25
 TE_COLS = SLICE * SLICES
-HALF = SLICES // 2
+GROUP = 4
+GROUPS = -(-SLICES // GROUP)
 AHEAD = 12
 TE = 0
 VE = 1
+STEPS = [[(VE, 0)], [(VE, 1)], [(VE, 2)], [(VE, 3), (TE, 0), (TE, 1)], [(VE, 4), (TE, 2), (TE, 3)], [(VE, 5), (TE, 4), (TE, 5)], [(TE, 6), (TE, 7)], [(VE, 6), (VE, 7)]]
+PLAN = {(VE,0,"v"):"SVVV",(VE,1,"v"):"SVVV",(VE,2,"k"):"GGVV",(VE,2,"v"):"GGGG",(TE,1,"k"):"GGVV",(TE,1,"v"):"GGGG",(TE,3,"k"):"GGGG",(TE,3,"v"):"GGGG",(TE,5,"k"):"GGGG",(TE,5,"v"):"GGGG",(TE,7,"k"):"GGGG",(TE,7,"v"):"GGGG",(VE,7,"v"):"GGGG",(VE,7,"k"):"SSVV",(VE,0,"k"):"SSVV",(VE,1,"k"):"SSVV"}
+GATED = [(VE,1),(VE,2),(TE,1),(TE,3),(TE,5),(TE,7),(VE,7)]
+PIECE = {(VE,0):2,(VE,1):2}
+RG = {0:[(VE,1,"k","V"),(VE,1,"v","V")],1:[(VE,2,"k","G"),(VE,2,"v","G"),(VE,2,"k","V"),(VE,3,"k","S"),(VE,3,"v","S")],2:[(TE,1,"k","G"),(TE,1,"v","G"),(TE,1,"k","V"),(TE,0,"k","S"),(TE,0,"v","S"),(VE,4,"k","S"),(VE,4,"v","S")],3:[(TE,2,"k","S"),(TE,2,"v","S"),(TE,3,"k","G"),(TE,3,"v","G"),(VE,5,"k","S"),(VE,5,"v","S")],4:[(TE,4,"k","S"),(TE,4,"v","S"),(TE,5,"k","G"),(TE,5,"v","G"),(TE,6,"k","S"),(TE,6,"v","S")],5:[(TE,7,"k","G"),(TE,7,"v","G"),(VE,6,"k","S"),(VE,6,"v","S"),(VE,7,"k","S")],6:[(VE,7,"v","G"),(VE,7,"k","V")],-1:[(VE,0,"k","V"),(VE,0,"k","S"),(VE,0,"v","V"),(VE,0,"v","S"),(VE,1,"k","S"),(VE,1,"v","S")],(3,"a"):[]}
+CARRY = {3:4,4:8,5:8,6:4}
+FLIPS = {6:[(0,"f"),(1,"f"),(2,"f"),(0,"m"),(1,"m"),(0,"s")],7:[(3,"f"),(4,"f"),(2,"m"),(3,"m"),(1,"s"),(5,"f"),(6,"f"),(4,"m"),(5,"m"),(2,"s"),(6,"m"),(3,"s")]}
+STORES = {}
 
 FLOPS = 2 * HEADS * WINDOWS * 512 * D * D + 2 * HEADS * WINDOWS * WINDOWS * D * D
 
@@ -45,177 +55,168 @@ def tile_mhla_pa_kernel(tc, k_feat, v, w_piece, out):
         psum_s = ctx.enter_context(tc.psum_pool(name="psum_s", bufs=5))
         ctx.enter_context(tc.manual_schedule())
 
-        steps = [[(VE, 0)], [(VE, 1)], [(VE, 2)]]
-        for a in range(WINDOWS // 2):
-            steps.append([(VE, a + 3), (TE, 2 * a), (TE, 2 * a + 1)])
-        steps.append([(VE, WINDOWS - 1)])
-        units = [unit for step in steps for unit in step]
-        te_end = 2 + WINDOWS // 2
-        ring_units = [step[-1] for step in steps[1:]]
-
+        units = [unit for step in STEPS for unit in step]
         raws = {}
         grps = {}
         words = {}
         banks = {}
+        flipped = {}
 
         def load(n):
             q, j = units[n]
             for name, src in (("k", k_feat), ("v", v)):
                 raw = rawp.tile([P, QUAD, ROW], BF16, tag="raw", name="raw_%s%d%d" % (name, q, j))
-                nc.sync.dma_start(
-                    out=raw[:],
-                    in_=src[0, QUAD * q : QUAD * (q + 1), j].rearrange("h (p t) d -> p h (t d)", t=PACK),
-                )
                 raws[(name, q, j)] = raw
-
-        def regroup(name, q, j):
-            raw = raws[(name, q, j)]
-            in_ring = (q, j) in ring_units
-            pool = grp_a if in_ring else grp_b
-            grp = pool.tile([P, QUAD, ROW], BF16, tag="grp", name="grp_%s%d%d" % (name, q, j), align_bytes=64)
-            grps[(name, q, j)] = grp
-            start = q == VE and j < 2
-            if (start and name == "k") or not (start or in_ring):
-                for h in range(QUAD):
-                    nc.scalar.copy(
-                        out=grp[:, h, :].rearrange("p (c i t) -> p c t i", i=4, t=PACK),
-                        in_=raw[:, h, :].rearrange("p (t c i) -> p c t i", i=4, t=PACK),
+                w = PIECE.get((q, j), QUAD)
+                for h in range(0, QUAD, w):
+                    nc.sync.dma_start(
+                        out=raw[:, h : h + w],
+                        in_=src[0, QUAD * q + h : QUAD * q + h + w, j].rearrange("h (p t) d -> p h (t d)", t=PACK),
                     )
-            elif start:
-                nc.vector.tensor_copy(
-                    out=grp[:].rearrange("p h (c i t) -> p h c t i", i=4, t=PACK),
-                    in_=raw[:].rearrange("p h (t c i) -> p h c t i", i=4, t=PACK),
+
+        def regroup(q, j, name, who):
+            raw = raws[(name, q, j)]
+            if (name, q, j) not in grps:
+                pool = grp_a if (q, j) in GATED else grp_b
+                grps[(name, q, j)] = pool.tile(
+                    [P, QUAD, ROW], BF16, tag="grp", name="grp_%s%d%d" % (name, q, j), align_bytes=64
                 )
-            else:
-                nc.gpsimd.tensor_scalar(
-                    out=grp[:].rearrange("p h (d t) -> p h d t", t=PACK),
-                    in0=raw[:].rearrange("p h (t d) -> p h d t", t=PACK),
-                    scalar1=1.0,
-                    scalar2=0.0,
-                    op0=MULT,
-                    op1=ADD,
+            grp = grps[(name, q, j)]
+            plan = PLAN.get((q, j, name), "SSSS")
+            h = 0
+            while h < QUAD:
+                n = 1
+                while plan[h] != "S" and h + n < QUAD and plan[h + n] == plan[h]:
+                    n += 1
+                if plan[h] == who:
+                    if who == "G":
+                        nc.gpsimd.tensor_scalar(
+                            out=grp[:, h : h + n].rearrange("p h (d t) -> p h d t", t=PACK),
+                            in0=raw[:, h : h + n].rearrange("p h (t d) -> p h d t", t=PACK),
+                            scalar1=1.0,
+                            scalar2=0.0,
+                            op0=MULT,
+                            op1=ADD,
+                        )
+                    elif who == "V":
+                        nc.vector.tensor_copy(
+                            out=grp[:, h : h + n].rearrange("p h (c i t) -> p h c t i", i=4, t=PACK),
+                            in_=raw[:, h : h + n].rearrange("p h (t c i) -> p h c t i", i=4, t=PACK),
+                        )
+                    else:
+                        nc.scalar.copy(
+                            out=grp[:, h, :].rearrange("p (c i t) -> p c t i", i=4, t=PACK),
+                            in_=raw[:, h, :].rearrange("p (t c i) -> p c t i", i=4, t=PACK),
+                        )
+                h += n
+
+        def quantise(q, j):
+            for name in ("v", "k") if (q, j) in GATED else ("k", "v"):
+                codes = mxp.tile([P, QUAD * D], U32, tag="codes", name="codes_%s%d%d" % (name, q, j), align_bytes=64)
+                scales = mxp.tile([P, QUAD * D], U8, tag="scales", name="scales_%s%d%d" % (name, q, j), align_bytes=64)
+                nc.vector.quantize_mx(
+                    out=codes[:].bitcast(FP8X4),
+                    scales=scales[:],
+                    in_=grps[(name, q, j)][:].rearrange("p h x -> p (h x)"),
                 )
+                words[(name, q, j)] = (codes, scales)
 
-        def regroup_unit(q, j):
-            regroup("k", q, j)
-            regroup("v", q, j)
-
-        def regroup_early(s):
-            if len(steps[s]) > 1:
-                regroup_unit(*steps[s][0])
-
-        def regroup_late(s):
-            for q, j in steps[s][1:] if len(steps[s]) > 1 else steps[s]:
-                if (q, j) == (VE, 1):
-                    regroup("v", q, j)
-                else:
-                    regroup_unit(q, j)
-            for q, j in steps[s]:
-                n = units.index((q, j))
-                if n + AHEAD < len(units):
-                    load(n + AHEAD)
-
-        def quantise(name, q, j):
-            codes = mxp.tile([P, QUAD * D], U32, tag="codes", name="codes_%s%d%d" % (name, q, j), align_bytes=64)
-            scales = mxp.tile([P, QUAD * D], U8, tag="scales", name="scales_%s%d%d" % (name, q, j), align_bytes=64)
-            nc.vector.quantize_mx(
-                out=codes[:].bitcast(FP8X4),
-                scales=scales[:],
-                in_=grps[(name, q, j)][:].rearrange("p h x -> p (h x)"),
+        def multiply(q, j, h, where):
+            cols = slice(h * D, (h + 1) * D)
+            nc.tensor.matmul_mx(
+                out=where,
+                lhsT=words[("k", q, j)][0][:, cols].bitcast(FP8X4),
+                lhsT_scale=words[("k", q, j)][1][:, cols],
+                rhs=words[("v", q, j)][0][:, cols].bitcast(FP8X4),
+                rhs_scale=words[("v", q, j)][1][:, cols],
+                start=True,
+                stop=True,
             )
-            words[(name, q, j)] = (codes, scales)
-
-        def passes_into(q, j, bank):
-            for h in range(QUAD):
-                cols = slice(h * D, (h + 1) * D)
-                nc.tensor.matmul_mx(
-                    out=bank[:, h, :],
-                    lhsT=words[("k", q, j)][0][:, cols].bitcast(FP8X4),
-                    lhsT_scale=words[("k", q, j)][1][:, cols],
-                    rhs=words[("v", q, j)][0][:, cols].bitcast(FP8X4),
-                    rhs_scale=words[("v", q, j)][1][:, cols],
-                    start=True,
-                    stop=True,
-                )
 
         def weight(i, j):
             return w_f[:, i * WINDOWS + j : i * WINDOWS + j + 1]
 
-        def quantise_and_multiply(q, j):
-            lo = TE_COLS if q == TE else 0
-            for name in ("v", "k") if (q, j) in ring_units else ("k", "v"):
-                quantise(name, q, j)
-            if q == TE or j == 0:
-                for_scalar = psum_s.tile([P, QUAD, D], F32, tag="s", name="for_scalar%d%d" % (q, j))
-                passes_into(q, j, for_scalar)
-                if q == TE:
-                    nc.scalar.copy(
-                        out=states[:, :, :, j, :],
-                        in_=for_scalar[:].rearrange("p h (s r) -> p h s r", r=SLICE)[:, :, 0:SLICES, :],
-                    )
-                if j == 0:
-                    for i in range(WINDOWS):
-                        nc.scalar.activation(
-                            out=acc[q][:, i, :, lo:D], in_=for_scalar[:, :, lo:D], func=COPY, scale=weight(i, 0)
-                        )
+        def multiply_unit(q, j):
+            for_scalar = q == TE or j == 0
+            if for_scalar:
+                bank = psum_s.tile([P, COLS], F32, tag="s", name="for_scalar%d%d" % (q, j))
+                for h in range(QUAD):
+                    multiply(q, j, h, bank[:, h * D : (h + 1) * D])
+                banks[("s", q, j)] = bank
             if j > 0:
-                for_vector = psum_v.tile([P, QUAD, D], F32, tag="v", name="for_vector%d%d" % (q, j))
-                passes_into(q, j, for_vector)
-                banks[(q, j)] = for_vector
+                bank = psum_v.tile([P, COLS], F32, tag="v", name="for_vector%d%d" % (q, j))
+                for h in [QUAD - 1] if q == TE else range(QUAD):
+                    multiply(q, j, h, bank[:, h * D : (h + 1) * D])
+                banks[("v", q, j)] = bank
 
-        def vector_mix(q, j):
+        def empty(q, j):
             lo = TE_COLS if q == TE else 0
-            if j == 0:
-                return
-            for i in range(WINDOWS):
-                nc.vector.scalar_tensor_tensor(
-                    out=acc[q][:, i, :, lo:D],
-                    in0=banks[(q, j)][:, :, lo:D],
-                    scalar=weight(i, j),
-                    in1=acc[q][:, i, :, lo:D],
-                    op0=MULT,
-                    op1=ADD,
-                )
-                if q == VE and j == WINDOWS - 1:
-                    nc.sync.dma_start(
-                        out=out[0, QUAD : 2 * QUAD, i].rearrange("h d e -> d h e"), in_=acc[VE][:, i, :, :]
-                    )
-
-        flipped = {}
-
-        def flip(h):
-            for half in range(2):
-                y_ps = psum_s.tile([P, HALF, P], F32, tag="s", name="y_ps%d_%d" % (h, half))
-                for k in range(HALF):
-                    nc.tensor.transpose(
-                        y_ps[:, k, :], states[:, h, half * HALF + k, :, :].rearrange("p j r -> p (j r)"), ident[:]
-                    )
-                y_sb = ysbp.tile([P, HALF, P], F32, tag="y_sb", name="y_sb%d_%d" % (h, half))
-                nc.scalar.copy(out=y_sb[:], in_=y_ps[:])
-                flipped[(h, half)] = y_sb
-
-        def te_mix(h):
-            for half in range(2):
-                o_ps = psum_s.tile([P, HALF, P], F32, tag="s", name="o_ps%d_%d" % (h, half))
-                for k in range(HALF):
-                    nc.tensor.matmul(
-                        out=o_ps[:, k, :],
-                        lhsT=flipped[(h, half)][:, k, :],
-                        rhs=kron[:].rearrange("p i r -> p (i r)"),
-                        start=True,
-                        stop=True,
-                    )
-                lo = half * HALF * SLICE
+            if q == TE:
                 nc.scalar.copy(
-                    out=acc[TE][:, :, h, lo : lo + HALF * SLICE].rearrange("p i (s r) -> p i s r", r=SLICE),
-                    in_=o_ps[:].rearrange("p s (i r) -> p i s r", r=SLICE),
+                    out=states[:, :, j, :],
+                    in_=banks[("s", q, j)][:, 0:TE_COLS].rearrange("p (s r) -> p s r", r=SLICE),
+                )
+            if j == 0:
+                for i in range(WINDOWS):
+                    nc.scalar.activation(
+                        out=acc[q][:, i, lo:COLS], in_=banks[("s", q, j)][:, lo:COLS], func=COPY, scale=weight(i, 0)
+                    )
+
+        def mix_row(q, j, i):
+            lo = TE_COLS if q == TE else 0
+            nc.vector.scalar_tensor_tensor(
+                out=acc[q][:, i, lo:COLS],
+                in0=banks[("v", q, j)][:, lo:COLS],
+                scalar=weight(i, j),
+                in1=acc[q][:, i, lo:COLS],
+                op0=MULT,
+                op1=ADD,
+            )
+            if q == VE and j == WINDOWS - 1:
+                nc.sync.dma_start(
+                    out=out[0, QUAD : 2 * QUAD, i].rearrange("h d e -> d h e"),
+                    in_=acc[VE][:, i, :].rearrange("p (h e) -> p h e", e=D),
                 )
 
-        for n in range(AHEAD):
-            load(n)
+        def group_size(g):
+            return min(GROUP, SLICES - g * GROUP)
 
+        def flip(g):
+            n = group_size(g)
+            y_ps = psum_s.tile([P, GROUP, P], F32, tag="s", name="y_ps%d" % g)
+            for s in range(n):
+                nc.tensor.transpose(
+                    y_ps[:, s, :], states[:, g * GROUP + s, :, :].rearrange("p j r -> p (j r)"), ident[:]
+                )
+            y_sb = ysbp.tile([P, GROUP, P], F32, tag="y_sb", name="y_sb%d" % g)
+            nc.scalar.copy(out=y_sb[:, 0:n, :], in_=y_ps[:, 0:n, :])
+            flipped[g] = y_sb
+
+        def mix_group(g):
+            n = group_size(g)
+            o_ps = psum_s.tile([P, GROUP, P], F32, tag="s", name="o_ps%d" % g)
+            for s in range(n):
+                nc.tensor.matmul(
+                    out=o_ps[:, s, :],
+                    lhsT=flipped[g][:, s, :],
+                    rhs=kron[:].rearrange("p i r -> p (i r)"),
+                    start=True,
+                    stop=True,
+                )
+            lo = g * GROUP * SLICE
+            nc.scalar.copy(
+                out=acc[TE][:, :, lo : lo + n * SLICE].rearrange("p i (s r) -> p i s r", r=SLICE),
+                in_=o_ps[:, 0:n, :].rearrange("p s (i r) -> p i s r", r=SLICE),
+            )
+
+        def store(h):
+            nc.scalar.dma_start(out=out[0, h].rearrange("i d e -> d i e"), in_=acc[TE][:, :, h * D : (h + 1) * D])
+
+        load(0)
         w_bf = const.tile([P, WINDOWS * WINDOWS], BF16)
         nc.scalar.dma_start(out=w_bf[:], in_=w_piece.rearrange("i j -> (i j)").partition_broadcast(P))
+        for n in range(1, AHEAD):
+            load(n)
         w_f = const.tile([P, WINDOWS * WINDOWS], F32)
         nc.vector.tensor_copy(out=w_f[:], in_=w_bf[:])
         ident = const.tile([P, P], F32)
@@ -244,37 +245,40 @@ def tile_mhla_pa_kernel(tc, k_feat, v, w_piece, out):
             in1=column_of[:].unsqueeze(1).to_broadcast([P, WINDOWS, SLICE]),
             op=MULT,
         )
-
         acc = [
-            accp.tile([P, WINDOWS, QUAD, D], F32, name="acc_te"),
-            accp.tile([P, WINDOWS, QUAD, D], F32, name="acc_ve"),
+            accp.tile([P, WINDOWS, COLS], F32, name="acc_te"),
+            accp.tile([P, WINDOWS, COLS], F32, name="acc_ve"),
         ]
-        states = accp.tile([P, QUAD, SLICES, WINDOWS, SLICE], F32, name="states")
+        states = accp.tile([P, SLICES, WINDOWS, SLICE], F32, name="states")
 
-        regroup_late(0)
-        regroup("k", VE, 1)
-        for s, step in enumerate(steps):
-            if s + 1 < len(steps):
-                regroup_early(s + 1)
+        for x in RG.get(-1, []):
+            regroup(x[0], x[1], x[2], x[3])
+        carried = []
+        for s, step in enumerate(STEPS):
+            for x in RG.get((s, "a"), []):
+                regroup(x[0], x[1], x[2], x[3])
             for q, j in step:
-                quantise_and_multiply(q, j)
-            if s + 1 < len(steps):
-                regroup_late(s + 1)
-            tail_steps = range(0, 3) if s == te_end else range(3, QUAD + 1) if s == te_end + 1 else range(0)
-            for t in tail_steps:
-                if t < QUAD:
-                    flip(t)
-                if t >= 1:
-                    te_mix(t - 1)
-                    if s > te_end:
-                        nc.scalar.dma_start(
-                            out=out[0, t - 1].rearrange("i d e -> d i e"), in_=acc[TE][:, :, t - 1, :]
-                        )
+                quantise(q, j)
+                multiply_unit(q, j)
+                empty(q, j)
+            for x in RG.get(s, []):
+                regroup(x[0], x[1], x[2], x[3])
             for q, j in step:
-                vector_mix(q, j)
-            if s == te_end:
-                for t in tail_steps:
-                    if t >= 1:
-                        nc.sync.dma_start(
-                            out=out[0, t - 1].rearrange("i d e -> d i e"), in_=acc[TE][:, :, t - 1, :]
-                        )
+                n = units.index((q, j))
+                if n + AHEAD < len(units):
+                    load(n + AHEAD)
+            rows = carried
+            for q, j in step:
+                rows = rows + [(q, j, i) for i in range(WINDOWS)] if j else rows
+            if len(step) == 2 and step[1][0] == VE:
+                pair = [(q, j, i) for i in range(WINDOWS) for q, j in step]
+                rows = carried + pair[:1] + [pair[x] for y in range(1, 2 * WINDOWS - 2, 2) for x in (y + 1, y)] + pair[-1:]
+            keep = CARRY.get(s, 0)
+            carried = rows[len(rows) - keep :]
+            for q, j, i in rows[: len(rows) - keep]:
+                mix_row(q, j, i)
+            for g, what in FLIPS.get(s, []):
+                if what == "s":
+                    store(g)
+                else:
+                    (flip if what == "f" else mix_group)(g)

@@ -30,11 +30,12 @@ AHEAD = 12
 TE = 0
 VE = 1
 STEPS = [[(VE, 0)], [(VE, 1)], [(VE, 2)], [(VE, 3), (TE, 0), (TE, 1)], [(VE, 4), (TE, 2), (TE, 3)], [(VE, 5), (TE, 4), (TE, 5)], [(TE, 6), (TE, 7)], [(VE, 6), (VE, 7)]]
-PLAN = {(VE,0,"v"):"SVVV",(VE,1,"v"):"SVVV",(VE,2,"k"):"GGVV",(VE,2,"v"):"GGGG",(TE,1,"k"):"GGVV",(TE,1,"v"):"GGGG",(TE,3,"k"):"GGGG",(TE,3,"v"):"GGGG",(TE,5,"k"):"GGGG",(TE,5,"v"):"GGGG",(TE,7,"k"):"GGGG",(TE,7,"v"):"GGGG",(VE,7,"v"):"GGGG",(VE,7,"k"):"SSVV",(VE,0,"k"):"SSVV",(VE,1,"k"):"SSVV"}
+PLAN = {(VE,0,"v"):"SSVV",(VE,1,"v"):"VVVV",(VE,2,"k"):"GGVV",(VE,2,"v"):"GGGG",(TE,1,"k"):"GGVV",(TE,1,"v"):"GGGG",(TE,3,"k"):"GGGG",(TE,3,"v"):"GGGG",(TE,5,"k"):"GGGG",(TE,5,"v"):"GGGG",(TE,7,"k"):"GGGG",(TE,7,"v"):"GGGG",(VE,7,"v"):"GGGG",(VE,7,"k"):"SSVV",(VE,0,"k"):"SSVV",(VE,1,"k"):"SSVV"}
 GATED = [(VE,1),(VE,2),(TE,1),(TE,3),(TE,5),(TE,7),(VE,7)]
 PIECE = {(VE,0):2,(VE,1):2}
 RG = {0:[(VE,1,"k","V"),(VE,1,"v","V")],1:[(VE,2,"k","G"),(VE,2,"v","G"),(VE,2,"k","V"),(VE,3,"k","S"),(VE,3,"v","S")],2:[(TE,1,"k","G"),(TE,1,"v","G"),(TE,1,"k","V"),(TE,0,"k","S"),(TE,0,"v","S"),(VE,4,"k","S"),(VE,4,"v","S")],3:[(TE,2,"k","S"),(TE,2,"v","S"),(TE,3,"k","G"),(TE,3,"v","G"),(VE,5,"k","S"),(VE,5,"v","S")],4:[(TE,4,"k","S"),(TE,4,"v","S"),(TE,5,"k","G"),(TE,5,"v","G"),(TE,6,"k","S"),(TE,6,"v","S")],5:[(TE,7,"k","G"),(TE,7,"v","G"),(VE,6,"k","S"),(VE,6,"v","S"),(VE,7,"k","S")],6:[(VE,7,"v","G"),(VE,7,"k","V")],-1:[(VE,0,"k","V"),(VE,0,"k","S"),(VE,0,"v","V"),(VE,0,"v","S"),(VE,1,"k","S"),(VE,1,"v","S")],(3,"a"):[]}
-CARRY = {3:4,4:8,5:8,6:4}
+CARRY = {5:8,6:4}
+G_ROWS = {(VE,6):[6,7],(VE,7):[7]}
 FLIPS = {6:[(0,"f"),(1,"f"),(2,"f"),(0,"m"),(1,"m"),(0,"s")],7:[(3,"f"),(4,"f"),(2,"m"),(3,"m"),(1,"s"),(5,"f"),(6,"f"),(4,"m"),(5,"m"),(2,"s"),(6,"m"),(3,"s")]}
 STORES = {}
 
@@ -50,6 +51,7 @@ def tile_mhla_pa_kernel(tc, k_feat, v, w_piece, out):
         grp_b = ctx.enter_context(tc.tile_pool(name="grp_b", bufs=8))
         mxp = ctx.enter_context(tc.tile_pool(name="mxp", bufs=8))
         accp = ctx.enter_context(tc.tile_pool(name="accp", bufs=1))
+        kvp = ctx.enter_context(tc.tile_pool(name="kvp", bufs=2))
         ysbp = ctx.enter_context(tc.tile_pool(name="ysbp", bufs=4))
         psum_v = ctx.enter_context(tc.psum_pool(name="psum_v", bufs=3))
         psum_s = ctx.enter_context(tc.psum_pool(name="psum_s", bufs=5))
@@ -61,6 +63,7 @@ def tile_mhla_pa_kernel(tc, k_feat, v, w_piece, out):
         words = {}
         banks = {}
         flipped = {}
+        kvs = {}
 
         def load(n):
             q, j = units[n]
@@ -137,7 +140,7 @@ def tile_mhla_pa_kernel(tc, k_feat, v, w_piece, out):
             return w_f[:, i * WINDOWS + j : i * WINDOWS + j + 1]
 
         def multiply_unit(q, j):
-            for_scalar = q == TE or j == 0
+            for_scalar = q == TE or j == 0 or (q, j) in G_ROWS
             if for_scalar:
                 bank = psum_s.tile([P, COLS], F32, tag="s", name="for_scalar%d%d" % (q, j))
                 for h in range(QUAD):
@@ -162,6 +165,24 @@ def tile_mhla_pa_kernel(tc, k_feat, v, w_piece, out):
                         out=acc[q][:, i, lo:COLS], in_=banks[("s", q, j)][:, lo:COLS], func=COPY, scale=weight(i, 0)
                     )
 
+        def copy_for_gpsimd(q, j):
+            kv = kvp.tile([P, COLS], F32, tag="kv", name="kv%d" % j)
+            nc.scalar.copy(out=kv[:], in_=banks[("s", q, j)][:])
+            kvs[(q, j)] = kv
+
+        def gpsimd_row(q, j, i):
+            part = kvp.tile([P, COLS], F32, tag="part", name="part%d%d" % (j, i))
+            nc.gpsimd.tensor_scalar(
+                out=part[:], in0=kvs[(q, j)][:], scalar1=weight(i, j), scalar2=0.0, op0=MULT, op1=ADD
+            )
+            nc.gpsimd.tensor_tensor(out=acc[q][:, i, :], in0=part[:], in1=acc[q][:, i, :], op=ADD)
+
+        def store_row(i):
+            nc.sync.dma_start(
+                out=out[0, QUAD : 2 * QUAD, i].rearrange("h d e -> d h e"),
+                in_=acc[VE][:, i, :].rearrange("p (h e) -> p h e", e=D),
+            )
+
         def mix_row(q, j, i):
             lo = TE_COLS if q == TE else 0
             nc.vector.scalar_tensor_tensor(
@@ -173,10 +194,7 @@ def tile_mhla_pa_kernel(tc, k_feat, v, w_piece, out):
                 op1=ADD,
             )
             if q == VE and j == WINDOWS - 1:
-                nc.sync.dma_start(
-                    out=out[0, QUAD : 2 * QUAD, i].rearrange("h d e -> d h e"),
-                    in_=acc[VE][:, i, :].rearrange("p (h e) -> p h e", e=D),
-                )
+                store_row(i)
 
         def group_size(g):
             return min(GROUP, SLICES - g * GROUP)
@@ -275,8 +293,17 @@ def tile_mhla_pa_kernel(tc, k_feat, v, w_piece, out):
                 rows = carried + pair[:1] + [pair[x] for y in range(1, 2 * WINDOWS - 2, 2) for x in (y + 1, y)] + pair[-1:]
             keep = CARRY.get(s, 0)
             carried = rows[len(rows) - keep :]
+            for q, j in step:
+                if (q, j) in G_ROWS:
+                    copy_for_gpsimd(q, j)
+            for q, j in step:
+                for i in G_ROWS.get((q, j), []):
+                    gpsimd_row(q, j, i)
             for q, j, i in rows[: len(rows) - keep]:
-                mix_row(q, j, i)
+                if i not in G_ROWS.get((q, j), []):
+                    mix_row(q, j, i)
+            for i in G_ROWS.get(step[-1], []):
+                store_row(i)
             for g, what in FLIPS.get(s, []):
                 if what == "s":
                     store(g)

@@ -30,13 +30,15 @@ AHEAD = 12
 TE = 0
 VE = 1
 STEPS = [[(VE, 0)], [(VE, 1)], [(VE, 2)], [(VE, 3), (TE, 0), (TE, 1)], [(VE, 4), (TE, 2), (TE, 3)], [(VE, 5), (TE, 4), (TE, 5)], [(TE, 6), (TE, 7)], [(VE, 6), (VE, 7)]]
-PLAN = {(VE,0,"v"):"SSVV",(VE,1,"v"):"VVVV",(VE,2,"k"):"GGVV",(VE,2,"v"):"GGGG",(TE,1,"k"):"GGVV",(TE,1,"v"):"GGGG",(TE,3,"k"):"GGGG",(TE,3,"v"):"GGGG",(TE,5,"k"):"GGGG",(TE,5,"v"):"GGGG",(TE,7,"k"):"GGGG",(TE,7,"v"):"GGGG",(VE,7,"v"):"GGGG",(VE,7,"k"):"SSVV",(VE,0,"k"):"SSVV",(VE,1,"k"):"SSVV"}
-GATED = [(VE,1),(VE,2),(TE,1),(TE,3),(TE,5),(TE,7),(VE,7)]
+PLAN = {(VE,0,"k"):"SSVV",(VE,0,"v"):"SSVV",(VE,1,"k"):"SSVV",(VE,1,"v"):"VVVV",(VE,2,"k"):"GGVV",(VE,2,"v"):"GGGG",(TE,1,"k"):"GGVV",(TE,1,"v"):"GGGG",(TE,3,"k"):"GGGG",(TE,3,"v"):"GGGG",(TE,5,"k"):"GGGG",(TE,5,"v"):"GGGG",(TE,7,"k"):"GGGG",(TE,7,"v"):"GGGG",(VE,7,"k"):"SSVV",(VE,7,"v"):"GGGG"}
+GATED = [(VE,1,"k"),(VE,1,"v"),(VE,2,"k"),(VE,2,"v"),(TE,1,"k"),(TE,1,"v"),(TE,3,"k"),(TE,3,"v"),(TE,5,"k"),(TE,5,"v"),(TE,7,"k"),(TE,7,"v"),(VE,7,"v")]
 PIECE = {(VE,0):2,(VE,1):2}
-RG = {0:[(VE,1,"k","V"),(VE,1,"v","V")],1:[(VE,2,"k","G"),(VE,2,"v","G"),(VE,2,"k","V"),(VE,3,"k","S"),(VE,3,"v","S")],2:[(TE,1,"k","G"),(TE,1,"v","G"),(TE,1,"k","V"),(TE,0,"k","S"),(TE,0,"v","S"),(VE,4,"k","S"),(VE,4,"v","S")],3:[(TE,2,"k","S"),(TE,2,"v","S"),(TE,3,"k","G"),(TE,3,"v","G"),(VE,5,"k","S"),(VE,5,"v","S")],4:[(TE,4,"k","S"),(TE,4,"v","S"),(TE,5,"k","G"),(TE,5,"v","G"),(TE,6,"k","S"),(TE,6,"v","S")],5:[(TE,7,"k","G"),(TE,7,"v","G"),(VE,6,"k","S"),(VE,6,"v","S"),(VE,7,"k","S")],6:[(VE,7,"v","G"),(VE,7,"k","V")],-1:[(VE,0,"k","V"),(VE,0,"k","S"),(VE,0,"v","V"),(VE,0,"v","S"),(VE,1,"k","S"),(VE,1,"v","S")],(3,"a"):[]}
+RG = {-1:[(VE,0,"k","V"),(VE,0,"k","S"),(VE,0,"v","V"),(VE,0,"v","S"),(VE,1,"k","S"),(VE,1,"v","S")],0:[(VE,1,"k","V"),(VE,1,"v","V")],1:[(VE,2,"k","V"),(VE,2,"k","T"),(VE,2,"k","G"),(VE,2,"v","G"),(VE,3,"k","S"),(VE,3,"v","S")],2:[(TE,1,"k","V"),(TE,1,"k","T"),(TE,1,"k","G"),(TE,1,"v","G"),(TE,0,"k","S"),(TE,0,"v","S"),(VE,4,"k","S"),(VE,4,"v","S")],3:[(TE,3,"k","G"),(TE,3,"v","G"),(TE,2,"k","S"),(TE,2,"v","S"),(VE,5,"k","S"),(VE,5,"v","S")],4:[(TE,5,"k","G"),(TE,5,"v","G"),(TE,4,"k","S"),(TE,4,"v","S"),(TE,6,"k","S"),(TE,6,"v","S")],5:[(TE,7,"k","G"),(TE,7,"v","G"),(VE,6,"k","S"),(VE,6,"v","S"),(VE,7,"k","S")],6:[(VE,7,"k","V"),(VE,7,"k","T"),(VE,7,"v","G")]}
 CARRY = {5:8,6:4}
 G_ROWS = {(VE,6):[6,7],(VE,7):[7]}
-FLIPS = {6:[(0,"f"),(1,"f"),(2,"f"),(0,"m"),(1,"m"),(0,"s")],7:[(3,"f"),(4,"f"),(2,"m"),(3,"m"),(1,"s"),(5,"f"),(6,"f"),(4,"m"),(5,"m"),(2,"s"),(6,"m"),(3,"s")]}
+WARM = {(TE,6):1,(TE,7):1,0:2}
+BETWEEN = {}
+FLIPS = {6:[(0,"f"),(1,"f"),(0,"m"),(2,"f"),(1,"m"),(0,"s")],7:[(3,"f"),(2,"m"),(4,"f"),(3,"m"),(1,"s"),(5,"f"),(4,"m"),(6,"f"),(5,"m"),(2,"s"),(6,"m"),(3,"s")]}
 STORES = {}
 
 FLOPS = 2 * HEADS * WINDOWS * 512 * D * D + 2 * HEADS * WINDOWS * WINDOWS * D * D
@@ -51,6 +53,7 @@ def tile_mhla_pa_kernel(tc, k_feat, v, w_piece, out):
         grp_b = ctx.enter_context(tc.tile_pool(name="grp_b", bufs=8))
         mxp = ctx.enter_context(tc.tile_pool(name="mxp", bufs=8))
         accp = ctx.enter_context(tc.tile_pool(name="accp", bufs=1))
+        gatep = ctx.enter_context(tc.tile_pool(name="gatep", bufs=2))
         kvp = ctx.enter_context(tc.tile_pool(name="kvp", bufs=2))
         ysbp = ctx.enter_context(tc.tile_pool(name="ysbp", bufs=4))
         psum_v = ctx.enter_context(tc.psum_pool(name="psum_v", bufs=3))
@@ -62,6 +65,7 @@ def tile_mhla_pa_kernel(tc, k_feat, v, w_piece, out):
         grps = {}
         words = {}
         banks = {}
+        gates = {}
         flipped = {}
         kvs = {}
 
@@ -78,9 +82,13 @@ def tile_mhla_pa_kernel(tc, k_feat, v, w_piece, out):
                     )
 
         def regroup(q, j, name, who):
+            if who == "T":
+                gates[(q, j)] = gatep.tile([P, 1], F32, tag="gate", name="gate%d%d" % (q, j))
+                nc.vector.tensor_copy(out=gates[(q, j)][:], in_=one[:])
+                return
             raw = raws[(name, q, j)]
             if (name, q, j) not in grps:
-                pool = grp_a if (q, j) in GATED else grp_b
+                pool = grp_a if (q, j, name) in GATED else grp_b
                 grps[(name, q, j)] = pool.tile(
                     [P, QUAD, ROW], BF16, tag="grp", name="grp_%s%d%d" % (name, q, j), align_bytes=64
                 )
@@ -96,7 +104,7 @@ def tile_mhla_pa_kernel(tc, k_feat, v, w_piece, out):
                         nc.gpsimd.tensor_scalar(
                             out=grp[:, h : h + n].rearrange("p h (d t) -> p h d t", t=PACK),
                             in0=raw[:, h : h + n].rearrange("p h (t d) -> p h d t", t=PACK),
-                            scalar1=1.0,
+                            scalar1=gates[(q, j)][:] if (q, j) in gates else 1.0,
                             scalar2=0.0,
                             op0=MULT,
                             op1=ADD,
@@ -114,7 +122,7 @@ def tile_mhla_pa_kernel(tc, k_feat, v, w_piece, out):
                 h += n
 
         def quantise(q, j):
-            for name in ("v", "k") if (q, j) in GATED else ("k", "v"):
+            for name in ("v", "k") if (q, j) == (TE, 7) else ("k", "v"):
                 codes = mxp.tile([P, QUAD * D], U32, tag="codes", name="codes_%s%d%d" % (name, q, j), align_bytes=64)
                 scales = mxp.tile([P, QUAD * D], U8, tag="scales", name="scales_%s%d%d" % (name, q, j), align_bytes=64)
                 nc.vector.quantize_mx(
@@ -123,6 +131,8 @@ def tile_mhla_pa_kernel(tc, k_feat, v, w_piece, out):
                     in_=grps[(name, q, j)][:].rearrange("p h x -> p (h x)"),
                 )
                 words[(name, q, j)] = (codes, scales)
+                for x in BETWEEN.get((q, j, name), []):
+                    regroup(x[0], x[1], x[2], x[3])
 
         def multiply(q, j, h, where):
             cols = slice(h * D, (h + 1) * D)
@@ -136,6 +146,17 @@ def tile_mhla_pa_kernel(tc, k_feat, v, w_piece, out):
                 stop=True,
             )
 
+        def warm_up(q, j, name, bank):
+            nc.tensor.matmul_mx(
+                out=bank,
+                lhsT=words[(name, q, j)][0][:, 0:D].bitcast(FP8X4),
+                lhsT_scale=words[(name, q, j)][1][:, 0:D],
+                rhs=words[(name, q, j)][0][:].bitcast(FP8X4),
+                rhs_scale=words[(name, q, j)][1][:],
+                start=True,
+                stop=True,
+            )
+
         def weight(i, j):
             return w_f[:, i * WINDOWS + j : i * WINDOWS + j + 1]
 
@@ -143,6 +164,8 @@ def tile_mhla_pa_kernel(tc, k_feat, v, w_piece, out):
             for_scalar = q == TE or j == 0 or (q, j) in G_ROWS
             if for_scalar:
                 bank = psum_s.tile([P, COLS], F32, tag="s", name="for_scalar%d%d" % (q, j))
+                for x in range(WARM.get((q, j), 0)):
+                    warm_up(q, j, "v" if (q, j) == (TE, 7) else "k", bank[:])
                 for h in range(QUAD):
                     multiply(q, j, h, bank[:, h * D : (h + 1) * D])
                 banks[("s", q, j)] = bank
@@ -213,6 +236,8 @@ def tile_mhla_pa_kernel(tc, k_feat, v, w_piece, out):
         def mix_group(g):
             n = group_size(g)
             o_ps = psum_s.tile([P, GROUP, P], F32, tag="s", name="o_ps%d" % g)
+            for x in range(WARM.get(g, 0)):
+                warm_up(TE, WINDOWS - 1, "k", o_ps[:].rearrange("p s d -> p (s d)"))
             for s in range(n):
                 nc.tensor.matmul(
                     out=o_ps[:, s, :],
@@ -263,6 +288,8 @@ def tile_mhla_pa_kernel(tc, k_feat, v, w_piece, out):
             in1=column_of[:].unsqueeze(1).to_broadcast([P, WINDOWS, SLICE]),
             op=MULT,
         )
+        one = const.tile([P, 1], F32)
+        nc.gpsimd.memset(one[:], 1.0)
         acc = [
             accp.tile([P, WINDOWS, COLS], F32, name="acc_te"),
             accp.tile([P, WINDOWS, COLS], F32, name="acc_ve"),

@@ -33,12 +33,12 @@ STEPS = [[(VE, 0)], [(VE, 1)], [(VE, 2)], [(VE, 3), (TE, 0), (TE, 1)], [(VE, 4),
 PLAN = {(VE,0,"k"):"SSVV",(VE,0,"v"):"SSVV",(VE,1,"k"):"SSVV",(VE,1,"v"):"VVVV",(VE,2,"k"):"GGVV",(VE,2,"v"):"GGGG",(TE,1,"k"):"GGVV",(TE,1,"v"):"GGGG",(TE,3,"k"):"GGGG",(TE,3,"v"):"GGGG",(TE,5,"k"):"GGGG",(TE,5,"v"):"GGGG",(TE,7,"k"):"GGGG",(TE,7,"v"):"GGGG",(VE,7,"k"):"SSVV",(VE,7,"v"):"GGGG"}
 GATED = [(VE,1,"k"),(VE,1,"v"),(VE,2,"k"),(VE,2,"v"),(TE,1,"k"),(TE,1,"v"),(TE,3,"k"),(TE,3,"v"),(TE,5,"k"),(TE,5,"v"),(TE,7,"k"),(TE,7,"v"),(VE,7,"v")]
 PIECE = {(VE,0):2,(VE,1):2}
-RG = {-1:[(VE,0,"k","V"),(VE,0,"k","S"),(VE,0,"v","V"),(VE,0,"v","S"),(VE,1,"k","S"),(VE,1,"v","S")],0:[(VE,1,"k","V"),(VE,1,"v","V")],1:[(VE,2,"k","V"),(VE,2,"k","T"),(VE,2,"k","G"),(VE,2,"v","G"),(VE,3,"k","S"),(VE,3,"v","S")],2:[(TE,1,"k","V"),(TE,1,"k","T"),(TE,1,"k","G"),(TE,1,"v","G"),(TE,0,"k","S"),(TE,0,"v","S"),(VE,4,"k","S"),(VE,4,"v","S")],3:[(TE,3,"k","G"),(TE,3,"v","G"),(TE,2,"k","S"),(TE,2,"v","S"),(VE,5,"k","S"),(VE,5,"v","S")],4:[(TE,5,"k","G"),(TE,5,"v","G"),(TE,4,"k","S"),(TE,4,"v","S"),(TE,6,"k","S"),(TE,6,"v","S")],5:[(TE,7,"k","G"),(TE,7,"v","G"),(VE,6,"k","S"),(VE,6,"v","S"),(VE,7,"k","S")],6:[(VE,7,"k","V"),(VE,7,"k","T"),(VE,7,"v","G")]}
+RG = {-1:[(VE,0,"k","V"),(VE,0,"k","S"),(VE,0,"v","V"),(VE,0,"v","S"),(VE,1,"k","S"),(VE,1,"v","S")],0:[(VE,1,"k","V"),(VE,1,"v","V")],1:[(VE,2,"k","V"),(VE,2,"k","T"),(VE,2,"k","G"),(VE,2,"v","G"),(VE,3,"k","S"),(VE,3,"v","S")],2:[(TE,1,"k","V"),(TE,1,"k","T"),(TE,1,"k","G"),(TE,1,"v","G"),(TE,0,"k","S"),(TE,0,"v","S"),(VE,4,"k","S"),(VE,4,"v","S")],3:[(TE,3,"k","G"),(TE,3,"v","G"),(TE,2,"k","S"),(TE,2,"v","S"),(VE,5,"k","S"),(VE,5,"v","S")],4:[(TE,5,"k","G"),(TE,5,"v","G"),(TE,4,"k","S"),(TE,4,"v","S"),(TE,6,"k","S"),(TE,6,"v","S")],5:[(TE,7,"k","G"),(TE,7,"v","G"),(VE,6,"k","S"),(VE,6,"v","S"),(VE,7,"k","S")],6:[(VE,7,"k","V"),(VE,7,"v","T"),(VE,7,"v","G")]}
 CARRY = {5:8,6:4}
 G_ROWS = {(VE,6):[6,7],(VE,7):[7]}
-WARM = {(TE,6):1,(TE,7):1,0:2}
+WARM = {99:0}
 BETWEEN = {}
-FLIPS = {6:[(0,"f"),(1,"f"),(0,"m"),(2,"f"),(1,"m"),(0,"s")],7:[(3,"f"),(2,"m"),(4,"f"),(3,"m"),(1,"s"),(5,"f"),(4,"m"),(6,"f"),(5,"m"),(2,"s"),(6,"m"),(3,"s")]}
+FLIPS = {6:[(6,"f"),(0,"f"),(1,"f"),(6,"m"),(0,"m"),(2,"f"),(1,"m"),(0,"s")],7:[(3,"s"),(3,"f"),(2,"m"),(4,"f"),(3,"m"),(1,"s"),(5,"f"),(4,"m"),(5,"m"),(2,"s")]}
 STORES = {}
 
 FLOPS = 2 * HEADS * WINDOWS * 512 * D * D + 2 * HEADS * WINDOWS * WINDOWS * D * D
@@ -53,7 +53,6 @@ def tile_mhla_pa_kernel(tc, k_feat, v, w_piece, out):
         grp_b = ctx.enter_context(tc.tile_pool(name="grp_b", bufs=8))
         mxp = ctx.enter_context(tc.tile_pool(name="mxp", bufs=8))
         accp = ctx.enter_context(tc.tile_pool(name="accp", bufs=1))
-        gatep = ctx.enter_context(tc.tile_pool(name="gatep", bufs=2))
         kvp = ctx.enter_context(tc.tile_pool(name="kvp", bufs=2))
         ysbp = ctx.enter_context(tc.tile_pool(name="ysbp", bufs=4))
         psum_v = ctx.enter_context(tc.psum_pool(name="psum_v", bufs=3))
@@ -65,7 +64,6 @@ def tile_mhla_pa_kernel(tc, k_feat, v, w_piece, out):
         grps = {}
         words = {}
         banks = {}
-        gates = {}
         flipped = {}
         kvs = {}
 
@@ -83,8 +81,11 @@ def tile_mhla_pa_kernel(tc, k_feat, v, w_piece, out):
 
         def regroup(q, j, name, who):
             if who == "T":
-                gates[(q, j)] = gatep.tile([P, 1], F32, tag="gate", name="gate%d%d" % (q, j))
-                nc.vector.tensor_copy(out=gates[(q, j)][:], in_=one[:])
+                if (name, q, j) not in grps:
+                    grps[(name, q, j)] = grp_a.tile(
+                        [P, QUAD, ROW], BF16, tag="grp", name="grp_%s%d%d" % (name, q, j), align_bytes=64
+                    )
+                nc.vector.tensor_copy(out=grps[(name, q, j)][:, 0, 0:2], in_=one[:])
                 return
             raw = raws[(name, q, j)]
             if (name, q, j) not in grps:
@@ -99,12 +100,14 @@ def tile_mhla_pa_kernel(tc, k_feat, v, w_piece, out):
                 n = 1
                 while plan[h] != "S" and h + n < QUAD and plan[h + n] == plan[h]:
                     n += 1
+                if plan[h] == "V" and n == 3:
+                    n = 2
                 if plan[h] == who:
                     if who == "G":
                         nc.gpsimd.tensor_scalar(
                             out=grp[:, h : h + n].rearrange("p h (d t) -> p h d t", t=PACK),
                             in0=raw[:, h : h + n].rearrange("p h (t d) -> p h d t", t=PACK),
-                            scalar1=gates[(q, j)][:] if (q, j) in gates else 1.0,
+                            scalar1=1.0,
                             scalar2=0.0,
                             op0=MULT,
                             op1=ADD,
@@ -288,8 +291,8 @@ def tile_mhla_pa_kernel(tc, k_feat, v, w_piece, out):
             in1=column_of[:].unsqueeze(1).to_broadcast([P, WINDOWS, SLICE]),
             op=MULT,
         )
-        one = const.tile([P, 1], F32)
-        nc.gpsimd.memset(one[:], 1.0)
+        one = const.tile([P, 2], BF16)
+        nc.gpsimd.memset(one[:], 0.0)
         acc = [
             accp.tile([P, WINDOWS, COLS], F32, name="acc_te"),
             accp.tile([P, WINDOWS, COLS], F32, name="acc_ve"),

@@ -125,7 +125,7 @@ def tile_mhla_pa_kernel(tc, k_feat, v, w_piece, out):
                 h += n
 
         def quantise(q, j):
-            for name in ("v", "k") if (q, j) == (TE, 7) else ("k", "v"):
+            for name in ("v", "k") if (q, j, "v") in GATED else ("k", "v"):
                 codes = mxp.tile([P, QUAD * D], U32, tag="codes", name="codes_%s%d%d" % (name, q, j), align_bytes=64)
                 scales = mxp.tile([P, QUAD * D], U8, tag="scales", name="scales_%s%d%d" % (name, q, j), align_bytes=64)
                 nc.vector.quantize_mx(

@@ -38,7 +38,7 @@ CARRY = {5:8,6:4}
 G_ROWS = {(VE,6):[6,7],(VE,7):[7]}
 WARM = {99:0}
 BETWEEN = {}
-FLIPS = {6:[(6,"f"),(0,"f"),(1,"f"),(6,"m"),(0,"m"),(2,"f"),(1,"m"),(0,"s")],7:[(3,"s"),(3,"f"),(2,"m"),(4,"f"),(3,"m"),(1,"s"),(5,"f"),(4,"m"),(5,"m"),(2,"s")]}
+FLIPS = {6:[(6,"f"),(0,"f"),(1,"f"),(2,"f"),(6,"m"),(0,"m"),(1,"m"),(0,"s")],7:[(3,"s"),(3,"f"),(4,"f"),(5,"f"),(2,"m"),(3,"m"),(1,"s"),(4,"m"),(5,"m"),(2,"s")]}
 STORES = {}
 
 FLOPS = 2 * HEADS * WINDOWS * 512 * D * D + 2 * HEADS * WINDOWS * WINDOWS * D * D

@@ -85,7 +85,7 @@ def tile_mhla_pa_kernel(tc, k_feat, v, w_piece, out):
                     grps[(name, q, j)] = grp_a.tile(
                         [P, QUAD, ROW], BF16, tag="grp", name="grp_%s%d%d" % (name, q, j), align_bytes=64
                     )
-                nc.vector.tensor_copy(out=grps[(name, q, j)][:, 0, 0:2], in_=one[:])
+                nc.vector.tensor_copy(out=grps[(name, q, j)][:, 0, 0:2], in_=w_bf[:, 0:2])
                 return
             raw = raws[(name, q, j)]
             if (name, q, j) not in grps:
@@ -291,8 +291,6 @@ def tile_mhla_pa_kernel(tc, k_feat, v, w_piece, out):
             in1=column_of[:].unsqueeze(1).to_broadcast([P, WINDOWS, SLICE]),
             op=MULT,
         )
-        one = const.tile([P, 2], BF16)
-        nc.gpsimd.memset(one[:], 0.0)
         acc = [
             accp.tile([P, WINDOWS, COLS], F32, name="acc_te"),
             accp.tile([P, WINDOWS, COLS], F32, name="acc_ve"),

@@ -70,7 +70,7 @@ def tile_mhla_pa_kernel(tc, k_feat, v, w_piece, out):
         def load(n):
             q, j = units[n]
             for name, src in (("k", k_feat), ("v", v)):
-                raw = rawp.tile([P, QUAD, ROW], BF16, tag="raw", name="raw_%s%d%d" % (name, q, j))
+                raw = rawp.tile([P, QUAD, ROW], BF16, tag="raw", name="raw_%s%d%d" % (name, q, j), align_bytes=512)
                 raws[(name, q, j)] = raw
                 w = PIECE.get((q, j), QUAD)
                 for h in range(0, QUAD, w):
@@ -83,7 +83,7 @@ def tile_mhla_pa_kernel(tc, k_feat, v, w_piece, out):
             if who == "T":
                 if (name, q, j) not in grps:
                     grps[(name, q, j)] = grp_a.tile(
-                        [P, QUAD, ROW], BF16, tag="grp", name="grp_%s%d%d" % (name, q, j), align_bytes=64
+                        [P, QUAD, ROW], BF16, tag="grp", name="grp_%s%d%d" % (name, q, j), align_bytes=512
                     )
                 nc.vector.tensor_copy(out=grps[(name, q, j)][:, 0, 0:2], in_=w_bf[:, 0:2])
                 return
@@ -91,7 +91,7 @@ def tile_mhla_pa_kernel(tc, k_feat, v, w_piece, out):
             if (name, q, j) not in grps:
                 pool = grp_a if (q, j, name) in GATED else grp_b
                 grps[(name, q, j)] = pool.tile(
-                    [P, QUAD, ROW], BF16, tag="grp", name="grp_%s%d%d" % (name, q, j), align_bytes=64
+                    [P, QUAD, ROW], BF16, tag="grp", name="grp_%s%d%d" % (name, q, j), align_bytes=512
                 )
             grp = grps[(name, q, j)]
             plan = PLAN.get((q, j, name), "SSSS")
@@ -126,8 +126,8 @@ def tile_mhla_pa_kernel(tc, k_feat, v, w_piece, out):
 
         def quantise(q, j):
             for name in ("v", "k") if (q, j, "v") in GATED else ("k", "v"):
-                codes = mxp.tile([P, QUAD * D], U32, tag="codes", name="codes_%s%d%d" % (name, q, j), align_bytes=64)
-                scales = mxp.tile([P, QUAD * D], U8, tag="scales", name="scales_%s%d%d" % (name, q, j), align_bytes=64)
+                codes = mxp.tile([P, QUAD * D], U32, tag="codes", name="codes_%s%d%d" % (name, q, j), align_bytes=512)
+                scales = mxp.tile([P, QUAD * D], U8, tag="scales", name="scales_%s%d%d" % (name, q, j), align_bytes=512)
                 nc.vector.quantize_mx(
                     out=codes[:].bitcast(FP8X4),
                     scales=scales[:],
@@ -192,12 +192,12 @@ def tile_mhla_pa_kernel(tc, k_feat, v, w_piece, out):
                     )
 
         def copy_for_gpsimd(q, j):
-            kv = kvp.tile([P, COLS], F32, tag="kv", name="kv%d" % j)
+            kv = kvp.tile([P, COLS], F32, tag="kv", name="kv%d" % j, align_bytes=512)
             nc.scalar.copy(out=kv[:], in_=banks[("s", q, j)][:])
             kvs[(q, j)] = kv
 
         def gpsimd_row(q, j, i):
-            part = kvp.tile([P, COLS], F32, tag="part", name="part%d%d" % (j, i))
+            part = kvp.tile([P, COLS], F32, tag="part", name="part%d%d" % (j, i), align_bytes=512)
             nc.gpsimd.tensor_scalar(
                 out=part[:], in0=kvs[(q, j)][:], scalar1=weight(i, j), scalar2=0.0, op0=MULT, op1=ADD
             )
@@ -232,7 +232,7 @@ def tile_mhla_pa_kernel(tc, k_feat, v, w_piece, out):
                 nc.tensor.transpose(
                     y_ps[:, s, :], states[:, g * GROUP + s, :, :].rearrange("p j r -> p (j r)"), ident[:]
                 )
-            y_sb = ysbp.tile([P, GROUP, P], F32, tag="y_sb", name="y_sb%d" % g)
+            y_sb = ysbp.tile([P, GROUP, P], F32, tag="y_sb", name="y_sb%d" % g, align_bytes=512)
             nc.scalar.copy(out=y_sb[:, 0:n, :], in_=y_ps[:, 0:n, :])
             flipped[g] = y_sb
 
@@ -292,10 +292,10 @@ def tile_mhla_pa_kernel(tc, k_feat, v, w_piece, out):
             op=MULT,
         )
         acc = [
-            accp.tile([P, WINDOWS, COLS], F32, name="acc_te"),
-            accp.tile([P, WINDOWS, COLS], F32, name="acc_ve"),
+            accp.tile([P, WINDOWS, COLS], F32, name="acc_te", align_bytes=512),
+            accp.tile([P, WINDOWS, COLS], F32, name="acc_ve", align_bytes=512),
         ]
-        states = accp.tile([P, SLICES, WINDOWS, SLICE], F32, name="states")
+        states = accp.tile([P, SLICES, WINDOWS, SLICE], F32, name="states", align_bytes=512)
 
         for x in RG.get(-1, []):
             regroup(x[0], x[1], x[2], x[3])

from contextlib import ExitStack

import concourse.mybir as mybir
from concourse.masks import make_identity

BF16 = mybir.dt.bfloat16
F32 = mybir.dt.float32
U32 = mybir.dt.uint32
U8 = mybir.dt.uint8
FP8X4 = mybir.dt.float8_e4m3fn_x4
MULT = mybir.AluOpType.mult
ADD = mybir.AluOpType.add
COPY = mybir.ActivationFunctionType.Copy
AXIS_X = mybir.AxisListType.X

P = 128
HEADS = 8
WINDOWS = 8
QUAD = 4
PACK = 4
D = 128
ROW = PACK * D
COLS = QUAD * D
SLICE = 16
SLICES = 25
TE_COLS = SLICE * SLICES
GROUP = 4
GROUPS = -(-SLICES // GROUP)
AHEAD = 12
TE = 0
VE = 1
STEPS = [[(VE, 0)], [(VE, 1)], [(VE, 2)], [(VE, 3), (TE, 0), (TE, 1)], [(VE, 4), (TE, 2), (TE, 3)], [(VE, 5), (TE, 4), (TE, 5)], [(TE, 6), (TE, 7)], [(VE, 6), (VE, 7)]]
PLAN = {(VE,0,"k"):"SSVV",(VE,0,"v"):"SSVV",(VE,1,"k"):"SSVV",(VE,1,"v"):"VVVV",(VE,2,"k"):"GGVV",(VE,2,"v"):"GGGG",(TE,1,"k"):"GGVV",(TE,1,"v"):"GGGG",(TE,3,"k"):"GGGG",(TE,3,"v"):"GGGG",(TE,5,"k"):"GGGG",(TE,5,"v"):"GGGG",(TE,7,"k"):"GGGG",(TE,7,"v"):"GGGG",(VE,7,"k"):"SSVV",(VE,7,"v"):"GGGG"}
GATED = [(VE,1,"k"),(VE,1,"v"),(VE,2,"k"),(VE,2,"v"),(TE,1,"k"),(TE,1,"v"),(TE,3,"k"),(TE,3,"v"),(TE,5,"k"),(TE,5,"v"),(TE,7,"k"),(TE,7,"v"),(VE,7,"v")]
PIECE = {(VE,0):2,(VE,1):2}
RG = {-1:[(VE,0,"k","V"),(VE,0,"k","S"),(VE,0,"v","V"),(VE,0,"v","S"),(VE,1,"k","S"),(VE,1,"v","S")],0:[(VE,1,"k","V"),(VE,1,"v","V")],1:[(VE,2,"k","V"),(VE,2,"k","T"),(VE,2,"k","G"),(VE,2,"v","G"),(VE,3,"k","S"),(VE,3,"v","S")],2:[(TE,1,"k","V"),(TE,1,"k","T"),(TE,1,"k","G"),(TE,1,"v","G"),(TE,0,"k","S"),(TE,0,"v","S"),(VE,4,"k","S"),(VE,4,"v","S")],3:[(TE,3,"k","G"),(TE,3,"v","G"),(TE,2,"k","S"),(TE,2,"v","S"),(VE,5,"k","S"),(VE,5,"v","S")],4:[(TE,5,"k","G"),(TE,5,"v","G"),(TE,4,"k","S"),(TE,4,"v","S"),(TE,6,"k","S"),(TE,6,"v","S")],5:[(TE,7,"k","G"),(TE,7,"v","G"),(VE,6,"k","S"),(VE,6,"v","S"),(VE,7,"k","S")],6:[(VE,7,"k","V"),(VE,7,"v","T"),(VE,7,"v","G")]}
CARRY = {5:8,6:4}
G_ROWS = {(VE,6):[6,7],(VE,7):[7]}
WARM = {99:0}
BETWEEN = {}
FLIPS = {6:[(6,"f"),(0,"f"),(1,"f"),(2,"f"),(6,"m"),(0,"m"),(1,"m"),(0,"s")],7:[(3,"s"),(3,"f"),(4,"f"),(5,"f"),(2,"m"),(3,"m"),(1,"s"),(4,"m"),(5,"m"),(2,"s")]}
STORES = {}

FLOPS = 2 * HEADS * WINDOWS * 512 * D * D + 2 * HEADS * WINDOWS * WINDOWS * D * D


def tile_mhla_pa_kernel(tc, k_feat, v, w_piece, out):
    nc = tc.nc
    with ExitStack() as ctx:
        const = ctx.enter_context(tc.tile_pool(name="const", bufs=1))
        rawp = ctx.enter_context(tc.tile_pool(name="rawp", bufs=2 * AHEAD))
        grp_a = ctx.enter_context(tc.tile_pool(name="grp_a", bufs=2))
        grp_b = ctx.enter_context(tc.tile_pool(name="grp_b", bufs=8))
        mxp = ctx.enter_context(tc.tile_pool(name="mxp", bufs=8))
        accp = ctx.enter_context(tc.tile_pool(name="accp", bufs=1))
        kvp = ctx.enter_context(tc.tile_pool(name="kvp", bufs=2))
        ysbp = ctx.enter_context(tc.tile_pool(name="ysbp", bufs=4))
        psum_v = ctx.enter_context(tc.psum_pool(name="psum_v", bufs=3))
        psum_s = ctx.enter_context(tc.psum_pool(name="psum_s", bufs=5))
        ctx.enter_context(tc.manual_schedule())

        units = [unit for step in STEPS for unit in step]
        raws = {}
        grps = {}
        words = {}
        banks = {}
        flipped = {}
        kvs = {}

        def load(n):
            q, j = units[n]
            for name, src in (("k", k_feat), ("v", v)):
                raw = rawp.tile([P, QUAD, ROW], BF16, tag="raw", name="raw_%s%d%d" % (name, q, j), align_bytes=512)
                raws[(name, q, j)] = raw
                w = PIECE.get((q, j), QUAD)
                for h in range(0, QUAD, w):
                    nc.sync.dma_start(
                        out=raw[:, h : h + w],
                        in_=src[0, QUAD * q + h : QUAD * q + h + w, j].rearrange("h (p t) d -> p h (t d)", t=PACK),
                    )

        def regroup(q, j, name, who):
            if who == "T":
                if (name, q, j) not in grps:
                    grps[(name, q, j)] = grp_a.tile(
                        [P, QUAD, ROW], BF16, tag="grp", name="grp_%s%d%d" % (name, q, j), align_bytes=512
                    )
                nc.vector.tensor_copy(out=grps[(name, q, j)][:, 0, 0:2], in_=w_bf[:, 0:2])
                return
            raw = raws[(name, q, j)]
            if (name, q, j) not in grps:
                pool = grp_a if (q, j, name) in GATED else grp_b
                grps[(name, q, j)] = pool.tile(
                    [P, QUAD, ROW], BF16, tag="grp", name="grp_%s%d%d" % (name, q, j), align_bytes=512
                )
            grp = grps[(name, q, j)]
            plan = PLAN.get((q, j, name), "SSSS")
            h = 0
            while h < QUAD:
                n = 1
                while plan[h] != "S" and h + n < QUAD and plan[h + n] == plan[h]:
                    n += 1
                if plan[h] == "V" and n == 3:
                    n = 2
                if plan[h] == who:
                    if who == "G":
                        nc.gpsimd.tensor_scalar(
                            out=grp[:, h : h + n].rearrange("p h (d t) -> p h d t", t=PACK),
                            in0=raw[:, h : h + n].rearrange("p h (t d) -> p h d t", t=PACK),
                            scalar1=1.0,
                            scalar2=0.0,
                            op0=MULT,
                            op1=ADD,
                        )
                    elif who == "V":
                        nc.vector.tensor_copy(
                            out=grp[:, h : h + n].rearrange("p h (c i t) -> p h c t i", i=4, t=PACK),
                            in_=raw[:, h : h + n].rearrange("p h (t c i) -> p h c t i", i=4, t=PACK),
                        )
                    else:
                        nc.scalar.copy(
                            out=grp[:, h, :].rearrange("p (c i t) -> p c t i", i=4, t=PACK),
                            in_=raw[:, h, :].rearrange("p (t c i) -> p c t i", i=4, t=PACK),
                        )
                h += n

        def quantise(q, j):
            for name in ("v", "k") if (q, j, "v") in GATED else ("k", "v"):
                codes = mxp.tile([P, QUAD * D], U32, tag="codes", name="codes_%s%d%d" % (name, q, j), align_bytes=512)
                scales = mxp.tile([P, QUAD * D], U8, tag="scales", name="scales_%s%d%d" % (name, q, j), align_bytes=512)
                nc.vector.quantize_mx(
                    out=codes[:].bitcast(FP8X4),
                    scales=scales[:],
                    in_=grps[(name, q, j)][:].rearrange("p h x -> p (h x)"),
                )
                words[(name, q, j)] = (codes, scales)
                for x in BETWEEN.get((q, j, name), []):
                    regroup(x[0], x[1], x[2], x[3])

        def multiply(q, j, h, where):
            cols = slice(h * D, (h + 1) * D)
            nc.tensor.matmul_mx(
                out=where,
                lhsT=words[("k", q, j)][0][:, cols].bitcast(FP8X4),
                lhsT_scale=words[("k", q, j)][1][:, cols],
                rhs=words[("v", q, j)][0][:, cols].bitcast(FP8X4),
                rhs_scale=words[("v", q, j)][1][:, cols],
                start=True,
                stop=True,
            )

        def warm_up(q, j, name, bank):
            nc.tensor.matmul_mx(
                out=bank,
                lhsT=words[(name, q, j)][0][:, 0:D].bitcast(FP8X4),
                lhsT_scale=words[(name, q, j)][1][:, 0:D],
                rhs=words[(name, q, j)][0][:].bitcast(FP8X4),
                rhs_scale=words[(name, q, j)][1][:],
                start=True,
                stop=True,
            )

        def weight(i, j):
            return w_f[:, i * WINDOWS + j : i * WINDOWS + j + 1]

        def multiply_unit(q, j):
            for_scalar = q == TE or j == 0 or (q, j) in G_ROWS
            if for_scalar:
                bank = psum_s.tile([P, COLS], F32, tag="s", name="for_scalar%d%d" % (q, j))
                for x in range(WARM.get((q, j), 0)):
                    warm_up(q, j, "v" if (q, j) == (TE, 7) else "k", bank[:])
                for h in range(QUAD):
                    multiply(q, j, h, bank[:, h * D : (h + 1) * D])
                banks[("s", q, j)] = bank
            if j > 0:
                bank = psum_v.tile([P, COLS], F32, tag="v", name="for_vector%d%d" % (q, j))
                for h in [QUAD - 1] if q == TE else range(QUAD):
                    multiply(q, j, h, bank[:, h * D : (h + 1) * D])
                banks[("v", q, j)] = bank

        def empty(q, j):
            lo = TE_COLS if q == TE else 0
            if q == TE:
                nc.scalar.copy(
                    out=states[:, :, j, :],
                    in_=banks[("s", q, j)][:, 0:TE_COLS].rearrange("p (s r) -> p s r", r=SLICE),
                )
            if j == 0:
                for i in range(WINDOWS):
                    nc.scalar.activation(
                        out=acc[q][:, i, lo:COLS], in_=banks[("s", q, j)][:, lo:COLS], func=COPY, scale=weight(i, 0)
                    )

        def copy_for_gpsimd(q, j):
            kv = kvp.tile([P, COLS], F32, tag="kv", name="kv%d" % j, align_bytes=512)
            nc.scalar.copy(out=kv[:], in_=banks[("s", q, j)][:])
            kvs[(q, j)] = kv

        def gpsimd_row(q, j, i):
            part = kvp.tile([P, COLS], F32, tag="part", name="part%d%d" % (j, i), align_bytes=512)
            nc.gpsimd.tensor_scalar(
                out=part[:], in0=kvs[(q, j)][:], scalar1=weight(i, j), scalar2=0.0, op0=MULT, op1=ADD
            )
            nc.gpsimd.tensor_tensor(out=acc[q][:, i, :], in0=part[:], in1=acc[q][:, i, :], op=ADD)

        def store_row(i):
            nc.sync.dma_start(
                out=out[0, QUAD : 2 * QUAD, i].rearrange("h d e -> d h e"),
                in_=acc[VE][:, i, :].rearrange("p (h e) -> p h e", e=D),
            )

        def mix_row(q, j, i):
            lo = TE_COLS if q == TE else 0
            nc.vector.scalar_tensor_tensor(
                out=acc[q][:, i, lo:COLS],
                in0=banks[("v", q, j)][:, lo:COLS],
                scalar=weight(i, j),
                in1=acc[q][:, i, lo:COLS],
                op0=MULT,
                op1=ADD,
            )
            if q == VE and j == WINDOWS - 1:
                store_row(i)

        def group_size(g):
            return min(GROUP, SLICES - g * GROUP)

        def flip(g):
            n = group_size(g)
            y_ps = psum_s.tile([P, GROUP, P], F32, tag="s", name="y_ps%d" % g)
            for s in range(n):
                nc.tensor.transpose(
                    y_ps[:, s, :], states[:, g * GROUP + s, :, :].rearrange("p j r -> p (j r)"), ident[:]
                )
            y_sb = ysbp.tile([P, GROUP, P], F32, tag="y_sb", name="y_sb%d" % g, align_bytes=512)
            nc.scalar.copy(out=y_sb[:, 0:n, :], in_=y_ps[:, 0:n, :])
            flipped[g] = y_sb

        def mix_group(g):
            n = group_size(g)
            o_ps = psum_s.tile([P, GROUP, P], F32, tag="s", name="o_ps%d" % g)
            for x in range(WARM.get(g, 0)):
                warm_up(TE, WINDOWS - 1, "k", o_ps[:].rearrange("p s d -> p (s d)"))
            for s in range(n):
                nc.tensor.matmul(
                    out=o_ps[:, s, :],
                    lhsT=flipped[g][:, s, :],
                    rhs=kron[:].rearrange("p i r -> p (i r)"),
                    start=True,
                    stop=True,
                )
            lo = g * GROUP * SLICE
            nc.scalar.copy(
                out=acc[TE][:, :, lo : lo + n * SLICE].rearrange("p i (s r) -> p i s r", r=SLICE),
                in_=o_ps[:, 0:n, :].rearrange("p s (i r) -> p i s r", r=SLICE),
            )

        def store(h):
            nc.scalar.dma_start(out=out[0, h].rearrange("i d e -> d i e"), in_=acc[TE][:, :, h * D : (h + 1) * D])

        load(0)
        w_bf = const.tile([P, WINDOWS * WINDOWS], BF16)
        nc.scalar.dma_start(out=w_bf[:], in_=w_piece.rearrange("i j -> (i j)").partition_broadcast(P))
        for n in range(1, AHEAD):
            load(n)
        w_f = const.tile([P, WINDOWS * WINDOWS], F32)
        nc.vector.tensor_copy(out=w_f[:], in_=w_bf[:])
        ident = const.tile([P, P], F32)
        make_identity(nc, ident[:])
        window_of = const.tile([P, WINDOWS], F32)
        nc.vector.tensor_reduce(
            out=window_of[:], in_=ident[:].rearrange("p (j r) -> p j r", r=SLICE), axis=AXIS_X, op=ADD
        )
        column_of = const.tile([P, SLICE], F32)
        nc.vector.tensor_reduce(
            out=column_of[:], in_=ident[:].rearrange("p (j r) -> p r j", r=SLICE), axis=AXIS_X, op=ADD
        )
        picked = const.tile([P, WINDOWS, WINDOWS], F32)
        nc.vector.tensor_tensor(
            out=picked[:],
            in0=w_f[:].rearrange("p (i j) -> p i j", j=WINDOWS),
            in1=window_of[:].unsqueeze(1).to_broadcast([P, WINDOWS, WINDOWS]),
            op=MULT,
        )
        w_own = const.tile([P, WINDOWS], F32)
        nc.vector.tensor_reduce(out=w_own[:], in_=picked[:], axis=AXIS_X, op=ADD)
        kron = const.tile([P, WINDOWS, SLICE], F32)
        nc.vector.tensor_tensor(
            out=kron[:],
            in0=w_own[:].unsqueeze(2).to_broadcast([P, WINDOWS, SLICE]),
            in1=column_of[:].unsqueeze(1).to_broadcast([P, WINDOWS, SLICE]),
            op=MULT,
        )
        acc = [
            accp.tile([P, WINDOWS, COLS], F32, name="acc_te", align_bytes=512),
            accp.tile([P, WINDOWS, COLS], F32, name="acc_ve", align_bytes=512),
        ]
        states = accp.tile([P, SLICES, WINDOWS, SLICE], F32, name="states", align_bytes=512)

        for x in RG.get(-1, []):
            regroup(x[0], x[1], x[2], x[3])
        carried = []
        for s, step in enumerate(STEPS):
            for x in RG.get((s, "a"), []):
                regroup(x[0], x[1], x[2], x[3])
            for q, j in step:
                quantise(q, j)
                multiply_unit(q, j)
                empty(q, j)
            for x in RG.get(s, []):
                regroup(x[0], x[1], x[2], x[3])
            for q, j in step:
                n = units.index((q, j))
                if n + AHEAD < len(units):
                    load(n + AHEAD)
            rows = carried
            for q, j in step:
                rows = rows + [(q, j, i) for i in range(WINDOWS)] if j else rows
            if len(step) == 2 and step[1][0] == VE:
                pair = [(q, j, i) for i in range(WINDOWS) for q, j in step]
                rows = carried + pair[:1] + [pair[x] for y in range(1, 2 * WINDOWS - 2, 2) for x in (y + 1, y)] + pair[-1:]
            keep = CARRY.get(s, 0)
            carried = rows[len(rows) - keep :]
            for q, j in step:
                if (q, j) in G_ROWS:
                    copy_for_gpsimd(q, j)
            for q, j in step:
                for i in G_ROWS.get((q, j), []):
                    gpsimd_row(q, j, i)
            for q, j, i in rows[: len(rows) - keep]:
                if i not in G_ROWS.get((q, j), []):
                    mix_row(q, j, i)
            for i in G_ROWS.get(step[-1], []):
                store_row(i)
            for g, what in FLIPS.get(s, []):
                if what == "s":
                    store(g)
                else:
                    (flip if what == "f" else mix_group)(g)
